import numpy as np
import ml_dtypes


def mxq(x, axis, fmt="e4m3"):
    dtype, down = {"e4m3": (ml_dtypes.float8_e4m3fn, 7), "e5m2": (ml_dtypes.float8_e5m2, 14)}[fmt]
    v = np.moveaxis(np.asarray(x, np.float32).astype(ml_dtypes.bfloat16).astype(np.float64), axis, -1)
    blocks = v.reshape(v.shape[:-1] + (-1, 32))
    amax = np.abs(blocks).max(-1, keepdims=True)
    byte = np.maximum(np.where(amax > 0, np.frexp(amax)[1] - 1 + 127, 0) - down, 1)
    scale = np.exp2(byte - 127.0)
    codes = (blocks / scale).astype(np.float32).astype(dtype).astype(np.float64)
    return np.moveaxis((codes * scale).reshape(v.shape), -1, axis)


WIDE = False


def mx_kscale(k):
    if not WIDE:
        return np.ones(k)
    levels = np.array([10, -10, 5, -5, 0])
    a = np.random.permutation(np.resize(levels, k // 512 * 4)).reshape(k // 512, 4)
    idx = np.arange(k)
    return np.exp2(a[idx // 512, idx % 128 // 32])


BF16 = ml_dtypes.bfloat16


def bf(x):
    return np.asarray(x, np.float32).astype(BF16)


def f64(x):
    return np.asarray(x).astype(np.float64)


E2M1 = np.array([0.0, 0.5, 1.0, 1.5, 2.0, 3.0, 4.0, 6.0, -0.0, -0.5, -1.0, -1.5, -2.0, -3.0, -4.0, -6.0])


def pack_weight(w, fmt):
    k, n = w.shape
    w = f64(bf(w)).reshape(k // 32, 32, n)
    amax = np.abs(w).max(1)
    if fmt == "e4m3":
        byte = np.frexp(amax)[1] - 1 + 127 - 7
    else:
        mant, ex = np.frexp(amax / 6.0)
        byte = np.where(mant > 0.5, ex, ex - 1) + 127
    byte = np.clip(np.where(amax > 0, byte, 1), 1, 254)
    scaled = (w * np.exp2(127.0 - byte)[:, None, :]).reshape(k, n).astype(np.float32)
    by_word = np.ascontiguousarray(scaled.reshape(k // 512, 128, 4, n).transpose(0, 1, 3, 2))
    if fmt == "e4m3":
        words = by_word.astype(ml_dtypes.float8_e4m3fn).view(np.uint8)
    else:
        c = by_word.astype(ml_dtypes.float4_e2m1fn).view(np.uint8) & 0xF
        words = c[..., 0::2] | (c[..., 1::2] << 4)
    return np.ascontiguousarray(words), np.ascontiguousarray(byte.astype(np.uint8).reshape(k // 512, 16, n))


def unpack_weight(words, scales, fmt):
    g, p, n, _ = words.shape
    if fmt == "e4m3":
        vals = np.ascontiguousarray(words).view(ml_dtypes.float8_e4m3fn).astype(np.float64)
    else:
        nib = np.empty((g, p, n, 4), np.uint8)
        nib[..., 0::2] = words & 0xF
        nib[..., 1::2] = words >> 4
        vals = E2M1[nib]
    vals = vals * np.repeat(np.exp2(scales.astype(np.float64) - 127.0), 8, axis=1)[..., None]
    return vals.transpose(0, 1, 3, 2).reshape(g * 512, n)

def pack4(w):
    words, scales = pack_weight(w, "e2m1")
    return words.reshape(words.shape[0], 128, -1), scales


def unpack4(words, scales):
    return unpack_weight(words.reshape(words.shape[0], 128, -1, 2), scales, "e2m1")


B, D, S, N = 1024, 2048, 4, 128
DS = D // S


def sigmoid(v):
    return 1.0 / (1.0 + np.exp(-v))


def setup_inputs():
    s = mx_kscale(D)
    t = np.maximum(1.0 + 2.0 * np.random.standard_normal((B, N, S)), 0.0) + np.maximum(1.0 + 2.0 * np.random.standard_normal((B, N, S)), 0.0)
    a = bf(t * t / (t * t).sum(axis=1, keepdims=True))
    vr = bf(np.random.standard_normal((N, S, DS)) * 0.5 * np.sqrt(N) * s.reshape(S, DS))
    h = bf(np.random.standard_normal((B, D)) * s)
    x2g = bf(np.random.standard_normal((B, D)))
    w_g = np.random.standard_normal((D, D)) / np.sqrt(D) / s
    w_g_words, w_g_scales = pack4(np.ascontiguousarray(w_g.T))
    b_g = bf(np.random.standard_normal(D) * 0.3)
    bg = bf(1.0 + 0.1 * np.random.standard_normal(1))
    return {"a": a,
            "vr": vr,
            "h": h,
            "x2g": x2g,
            "w_g_words": w_g_words,
            "w_g_scales": w_g_scales,
            "b_g": b_g,
            "bg": bg}


def reference(a, vr, h, x2g, w_g_words, w_g_scales, b_g, bg):
    hf = f64(h)
    hh = (f64(a).transpose(2, 0, 1) @ f64(vr).transpose(1, 0, 2)).transpose(1, 0, 2).reshape(B, D)
    h2g = (mxq(hf, 1, "e4m3") @ unpack4(w_g_words, w_g_scales)) + f64(b_g)
    g = sigmoid(f64(x2g) + h2g + f64(bg))
    return g * hh + (1.0 - g) * hf

@@ -1,0 +1,187 @@
+from contextlib import ExitStack
+
+import concourse.mybir as mybir
+from concourse.masks import make_identity
+
+F32 = mybir.dt.float32
+BF16 = mybir.dt.bfloat16
+I32 = mybir.dt.int32
+U32 = mybir.dt.uint32
+U8 = mybir.dt.uint8
+FP8X4 = mybir.dt.float8_e4m3fn_x4
+FP4X4 = mybir.dt.float4_e2m1fn_x4
+ADD = mybir.AluOpType.add
+SUBTRACT = mybir.AluOpType.subtract
+MULT = mybir.AluOpType.mult
+ACT = mybir.ActivationFunctionType
+
+P = 128
+B, D, S, ROLES = 1024, 2048, 4, 128
+SLICE = D // S
+K_PASS = 4 * P
+PASSES = D // K_PASS
+ROW_TILES = B // P
+
+FLOPS = 2 * B * D * D + 2 * B * ROLES * D
+
+
+def tile_tpru_pb_kernel(tc, a, vr, h, x2g, w_g_words, w_g_scales, b_g, bg, out):
+    nc = tc.nc
+    h_rows = h.rearrange("(i p) d -> i p d", p=P)
+    x2g_rows = x2g.rearrange("(i p) d -> i p d", p=P)
+    a_rows = a.rearrange("(i p) n s -> i p (n s)", p=P)
+    out_rows = out.rearrange("(i p) d -> i p d", p=P)
+
+    with ExitStack() as ctx:
+        const = ctx.enter_context(tc.tile_pool(name="const", bufs=1))
+        rows = ctx.enter_context(tc.tile_pool(name="rows", bufs=ROW_TILES))
+        prep = ctx.enter_context(tc.tile_pool(name="prep", bufs=3))
+        wide = ctx.enter_context(tc.tile_pool(name="wide", bufs=2))
+        work = ctx.enter_context(tc.tile_pool(name="work", bufs=4))
+        psum = ctx.enter_context(tc.psum_pool(name="psum", bufs=2))
+
+        w_planes = const.tile([P, PASSES, D], U8, align_bytes=64)
+        nc.vector.memset(w_planes[:].rearrange("p g n -> p (g n)").bitcast(I32), 0)
+
+        h_sb, x2g_sb, a_sb = [], [], []
+
+        def load_rows(i):
+            h_tile = rows.tile([P, D], BF16)
+            nc.sync.dma_start(out=h_tile[:], in_=h_rows[i])
+            h_sb.append(h_tile)
+            x2g_tile = rows.tile([P, D], BF16)
+            nc.sync.dma_start(out=x2g_tile[:], in_=x2g_rows[i])
+            x2g_sb.append(x2g_tile)
+            a_tile = rows.tile([P, ROLES * S], BF16)
+            nc.sync.dma_start(out=a_tile[:], in_=a_rows[i])
+            a_sb.append(a_tile)
+
+        load_rows(0)
+
+        bias_row = const.tile([P, D], BF16)
+        nc.vector.memset(bias_row[:], 0.0)
+        nc.sync.dma_start(out=bias_row[0:1, :], in_=b_g.unsqueeze(0))
+        bg_bf16 = const.tile([P, 1], BF16)
+        nc.sync.dma_start(out=bg_bf16[:], in_=bg.partition_broadcast(P))
+
+        scales_by_row = w_g_scales.rearrange("g q n -> q g n")
+        for first in range(8):
+            partition = 32 * (first // 4) + first % 4
+            nc.sync.dma_start(
+                out=w_planes[partition:P:64, :, :].bitcast(I32),
+                in_=scales_by_row[first:16:8].bitcast(I32),
+            )
+
+        w_words = const.tile([P, PASSES, 2 * D], U8, align_bytes=64)
+        words_by_partition = w_g_words.rearrange("g p c -> p g c")
+        vr_sb = const.tile([P, D], BF16)
+        for j in range(S):
+            word_cols = slice(2 * SLICE * j, 2 * SLICE * (j + 1))
+            nc.sync.dma_start(
+                out=w_words[:, :, word_cols].bitcast(I32),
+                in_=words_by_partition[:, :, word_cols].bitcast(I32),
+            )
+            if j == 0:
+                nc.sync.dma_start(out=vr_sb[:], in_=vr.rearrange("n s d -> n (s d)"))
+        for i in range(1, ROW_TILES):
+            load_rows(i)
+
+        ident = const.tile([P, P], F32)
+        make_identity(nc, ident[:])
+        ones = const.tile([P, P], BF16)
+        nc.vector.memset(ones[:], 1.0)
+        bg_f32 = const.tile([P, 1], F32)
+        nc.vector.tensor_copy(out=bg_f32[:], in_=bg_bf16[:])
+
+        bias_all = const.tile([P, D], F32)
+        for j in range(S):
+            cols = slice(SLICE * j, SLICE * (j + 1))
+            spread = psum.tile([P, SLICE], F32, tag="hh", bufs=3)
+            nc.tensor.matmul(spread[:], lhsT=ones[:], rhs=bias_row[:, cols], start=True, stop=True)
+            nc.scalar.activation(
+                out=bias_all[:, cols], in_=spread[:], func=ACT.Identity, bias=bg_f32[:, 0:1], scale=1.0
+            )
+
+        h_codes, h_planes, roles_t, gate_in = {}, {}, {}, {}
+
+        def transpose_and_quantise(i):
+            h_words = h_sb[i][:].bitcast(F32)
+            grouped = prep.tile([P, D], BF16, align_bytes=64)
+            grouped_words = grouped[:].bitcast(F32).rearrange("p (g b u) -> p g b u", g=PASSES, b=P, u=2)
+            for half in range(2):
+                flipped = psum.tile([P, 2, 2, P], F32, tag="tr", bufs=2)
+                for gg in range(2):
+                    g = 2 * half + gg
+                    for u in range(2):
+                        nc.tensor.transpose(
+                            flipped[:, gg, u, :], h_words[:, 256 * g + u : 256 * (g + 1) : 2], ident[:]
+                        )
+                nc.scalar.copy(
+                    out=grouped_words[:, 2 * half : 2 * half + 2, :, :],
+                    in_=flipped[:].rearrange("p g u b -> p g b u"),
+                )
+            a_words = a_sb[i][:].bitcast(F32)
+            a_flipped = psum.tile([P, 2, P], F32, tag="tr", bufs=2)
+            for u in range(2):
+                nc.tensor.transpose(a_flipped[:, u, :], a_words[:, u : 2 * ROLES : 2], ident[:])
+            a_t = prep.tile([P, S, P], BF16)
+            nc.scalar.copy(
+                out=a_t[:].rearrange("n (u e) b -> n u e b", u=2),
+                in_=a_flipped[:]
+                .rearrange("n u b -> n (u b)")
+                .bitcast(BF16)
+                .rearrange("n (u b e) -> n u e b", u=2, b=P, e=2),
+            )
+            roles_t[i] = a_t
+            codes = prep.tile([P, PASSES * P], U32, align_bytes=64)
+            planes = prep.tile([P, PASSES * P], U8, align_bytes=64)
+            nc.vector.quantize_mx(out=codes[:].bitcast(FP8X4), scales=planes[:], in_=grouped[:])
+            h_codes[i] = codes
+            h_planes[i] = planes
+            gate_in[i] = wide.tile([P, D], F32, name="gate_in")
+
+        def add_bias(i, j):
+            cols = slice(SLICE * j, SLICE * (j + 1))
+            nc.gpsimd.tensor_tensor(
+                out=gate_in[i][:, cols], in0=x2g_sb[i][:, cols], in1=bias_all[:, cols], op=ADD
+            )
+
+        def one_slice(i, j, blended):
+            cols = slice(SLICE * j, SLICE * (j + 1))
+            hh = psum.tile([P, SLICE], F32, tag="hh", bufs=3)
+            nc.tensor.matmul(hh[:], lhsT=roles_t[i][:, j, :], rhs=vr_sb[:, cols], start=True, stop=True)
+            logits = psum.tile([P, SLICE], F32, tag="acc", bufs=3)
+            for g in range(PASSES):
+                rows_g = slice(P * g, P * (g + 1))
+                nc.tensor.matmul_mx(
+                    out=logits[:],
+                    lhsT=h_codes[i][:, rows_g].bitcast(FP8X4),
+                    lhsT_scale=h_planes[i][:, rows_g],
+                    rhs=w_words[:, g, 2 * SLICE * j : 2 * SLICE * (j + 1)].bitcast(FP4X4),
+                    rhs_scale=w_planes[:, g, cols],
+                    start=(g == 0),
+                    stop=(g == PASSES - 1),
+                )
+            z = work.tile([P, SLICE], F32)
+            nc.vector.tensor_tensor(out=z[:], in0=logits[:], in1=gate_in[i][:, cols], op=ADD)
+            keep = work.tile([P, SLICE], F32)
+            nc.scalar.activation(out=keep[:], in_=z[:], func=ACT.Sigmoid, scale=-1.0)
+            diff = work.tile([P, SLICE], F32)
+            nc.vector.tensor_tensor(out=diff[:], in0=hh[:], in1=h_sb[i][:, cols], op=SUBTRACT)
+            back = work.tile([P, SLICE], F32)
+            multiplier = nc.vector if j == S - 1 else nc.gpsimd
+            multiplier.tensor_tensor(out=back[:], in0=keep[:], in1=diff[:], op=MULT)
+            nc.vector.tensor_tensor(out=blended[:, cols], in0=hh[:], in1=back[:], op=SUBTRACT)
+
+        transpose_and_quantise(0)
+        for j in range(S):
+            add_bias(0, j)
+        for i in range(ROW_TILES):
+            if i + 1 < ROW_TILES:
+                transpose_and_quantise(i + 1)
+            blended = wide.tile([P, D], F32)
+            for j in range(S):
+                one_slice(i, j, blended)
+                if i + 1 < ROW_TILES:
+                    add_bias(i + 1, j)
+            nc.sync.dma_start(out=out_rows[i], in_=blended[:])

@@ -25,6 +25,10 @@ ROW_TILES = B // P
 FLOPS = 2 * B * D * D + 2 * B * ROLES * D
 
 
+def vector_side(i):
+    return (2, 3) if i == 0 else (3,)
+
+
 def tile_tpru_pb_kernel(tc, a, vr, h, x2g, w_g_words, w_g_scales, b_g, bg, out):
     nc = tc.nc
     h_rows = h.rearrange("(i p) d -> i p d", p=P)
@@ -36,34 +40,38 @@ def tile_tpru_pb_kernel(tc, a, vr, h, x2g, w_g_words, w_g_scales, b_g, bg, out):
         const = ctx.enter_context(tc.tile_pool(name="const", bufs=1))
         rows = ctx.enter_context(tc.tile_pool(name="rows", bufs=ROW_TILES))
         prep = ctx.enter_context(tc.tile_pool(name="prep", bufs=3))
-        wide = ctx.enter_context(tc.tile_pool(name="wide", bufs=2))
-        work = ctx.enter_context(tc.tile_pool(name="work", bufs=4))
+        gates = ctx.enter_context(tc.tile_pool(name="gates", bufs=2))
+        outs = ctx.enter_context(tc.tile_pool(name="outs", bufs=3))
+        work = ctx.enter_context(tc.tile_pool(name="work", bufs=3))
         psum = ctx.enter_context(tc.psum_pool(name="psum", bufs=2))
+        ctx.enter_context(tc.manual_schedule())
 
         w_planes = const.tile([P, PASSES, D], U8, align_bytes=64)
         nc.vector.memset(w_planes[:].rearrange("p g n -> p (g n)").bitcast(I32), 0)
-
-        h_sb, x2g_sb, a_sb = [], [], []
-
-        def load_rows(i):
-            h_tile = rows.tile([P, D], BF16)
-            nc.sync.dma_start(out=h_tile[:], in_=h_rows[i])
-            h_sb.append(h_tile)
-            x2g_tile = rows.tile([P, D], BF16)
-            nc.sync.dma_start(out=x2g_tile[:], in_=x2g_rows[i])
-            x2g_sb.append(x2g_tile)
-            a_tile = rows.tile([P, ROLES * S], BF16)
-            nc.sync.dma_start(out=a_tile[:], in_=a_rows[i])
-            a_sb.append(a_tile)
-
-        load_rows(0)
-
         bias_row = const.tile([P, D], BF16)
-        nc.vector.memset(bias_row[:], 0.0)
+        nc.gpsimd.memset(bias_row[:], 0.0)
+        ones = const.tile([P, P], BF16)
+        nc.gpsimd.memset(ones[:], 1.0)
+        warm = const.tile([P, 2], F32)
+        nc.vector.memset(warm[:], 0.0)
+        nc.scalar.activation(out=warm[:, 1:2], in_=warm[:, 0:1], func=ACT.Sigmoid)
+
+        h_sb, x2g_sb, a_sb = {}, {}, {}
+
+        def load_h_a(i):
+            h_sb[i] = rows.tile([P, D], BF16, name="h_tile")
+            nc.sync.dma_start(out=h_sb[i][:], in_=h_rows[i])
+            a_sb[i] = rows.tile([P, ROLES * S], BF16, name="a_tile")
+            nc.sync.dma_start(out=a_sb[i][:], in_=a_rows[i])
+
+        def load_x2g(i):
+            x2g_sb[i] = rows.tile([P, D], BF16, name="x2g_tile")
+            nc.sync.dma_start(out=x2g_sb[i][:], in_=x2g_rows[i])
+
+        load_h_a(0)
         nc.sync.dma_start(out=bias_row[0:1, :], in_=b_g.unsqueeze(0))
         bg_bf16 = const.tile([P, 1], BF16)
         nc.sync.dma_start(out=bg_bf16[:], in_=bg.partition_broadcast(P))
-
         scales_by_row = w_g_scales.rearrange("g q n -> q g n")
         for first in range(8):
             partition = 32 * (first // 4) + first % 4
@@ -71,42 +79,53 @@ def tile_tpru_pb_kernel(tc, a, vr, h, x2g, w_g_words, w_g_scales, b_g, bg, out):
                 out=w_planes[partition:P:64, :, :].bitcast(I32),
                 in_=scales_by_row[first:16:8].bitcast(I32),
             )
-
         w_words = const.tile([P, PASSES, 2 * D], U8, align_bytes=64)
         words_by_partition = w_g_words.rearrange("g p c -> p g c")
         vr_sb = const.tile([P, D], BF16)
-        for j in range(S):
+
+        def load_w(j):
             word_cols = slice(2 * SLICE * j, 2 * SLICE * (j + 1))
             nc.sync.dma_start(
                 out=w_words[:, :, word_cols].bitcast(I32),
                 in_=words_by_partition[:, :, word_cols].bitcast(I32),
             )
-            if j == 0:
-                nc.sync.dma_start(out=vr_sb[:], in_=vr.rearrange("n s d -> n (s d)"))
-        for i in range(1, ROW_TILES):
-            load_rows(i)
+
+        load_w(0)
+        nc.sync.dma_start(out=vr_sb[:], in_=vr.rearrange("n s d -> n (s d)"))
+        load_h_a(1)
+        load_x2g(0)
+        load_x2g(1)
+        load_w(1)
+        load_w(2)
+        load_w(3)
+        for i in range(2, ROW_TILES):
+            load_h_a(i)
+            load_x2g(i)
 
         ident = const.tile([P, P], F32)
         make_identity(nc, ident[:])
-        ones = const.tile([P, P], BF16)
-        nc.vector.memset(ones[:], 1.0)
+        ident_bf16 = const.tile([P, P], BF16)
+        make_identity(nc, ident_bf16[:])
+        minus_ident = const.tile([P, P], BF16)
+        nc.vector.tensor_scalar_mul(out=minus_ident[:], in0=ident_bf16[:], scalar1=-1.0)
         bg_f32 = const.tile([P, 1], F32)
         nc.vector.tensor_copy(out=bg_f32[:], in_=bg_bf16[:])
 
         bias_all = const.tile([P, D], F32)
         for j in range(S):
             cols = slice(SLICE * j, SLICE * (j + 1))
-            spread = psum.tile([P, SLICE], F32, tag="hh", bufs=3)
+            spread = psum.tile([P, SLICE], F32, tag="acc", bufs=3)
             nc.tensor.matmul(spread[:], lhsT=ones[:], rhs=bias_row[:, cols], start=True, stop=True)
             nc.scalar.activation(
                 out=bias_all[:, cols], in_=spread[:], func=ACT.Identity, bias=bg_f32[:, 0:1], scale=1.0
             )
 
-        h_codes, h_planes, roles_t, gate_in = {}, {}, {}, {}
+        h_codes, h_planes, roles_t, grouped_of, gate, hh_of, acc_of, diff_sb = {}, {}, {}, {}, {}, {}, {}, {}
 
-        def transpose_and_quantise(i):
+        def transpose_h(i):
             h_words = h_sb[i][:].bitcast(F32)
-            grouped = prep.tile([P, D], BF16, align_bytes=64)
+            grouped = prep.tile([P, D], BF16, align_bytes=64, name="grouped")
+            grouped_of[i] = grouped
             grouped_words = grouped[:].bitcast(F32).rearrange("p (g b u) -> p g b u", g=PASSES, b=P, u=2)
             for half in range(2):
                 flipped = psum.tile([P, 2, 2, P], F32, tag="tr", bufs=2)
@@ -120,11 +139,13 @@ def tile_tpru_pb_kernel(tc, a, vr, h, x2g, w_g_words, w_g_scales, b_g, bg, out):
                     out=grouped_words[:, 2 * half : 2 * half + 2, :, :],
                     in_=flipped[:].rearrange("p g u b -> p g b u"),
                 )
+
+        def transpose_a(i):
             a_words = a_sb[i][:].bitcast(F32)
             a_flipped = psum.tile([P, 2, P], F32, tag="tr", bufs=2)
             for u in range(2):
                 nc.tensor.transpose(a_flipped[:, u, :], a_words[:, u : 2 * ROLES : 2], ident[:])
-            a_t = prep.tile([P, S, P], BF16)
+            a_t = prep.tile([P, S, P], BF16, name="a_t")
             nc.scalar.copy(
                 out=a_t[:].rearrange("n (u e) b -> n u e b", u=2),
                 in_=a_flipped[:]
@@ -133,55 +154,103 @@ def tile_tpru_pb_kernel(tc, a, vr, h, x2g, w_g_words, w_g_scales, b_g, bg, out):
                 .rearrange("n (u b e) -> n u e b", u=2, b=P, e=2),
             )
             roles_t[i] = a_t
-            codes = prep.tile([P, PASSES * P], U32, align_bytes=64)
-            planes = prep.tile([P, PASSES * P], U8, align_bytes=64)
-            nc.vector.quantize_mx(out=codes[:].bitcast(FP8X4), scales=planes[:], in_=grouped[:])
+
+        def quantise(i):
+            codes = prep.tile([P, PASSES * P], U32, align_bytes=64, name="codes")
+            planes = prep.tile([P, PASSES * P], U8, align_bytes=64, name="planes")
+            nc.vector.quantize_mx(out=codes[:].bitcast(FP8X4), scales=planes[:], in_=grouped_of[i][:])
             h_codes[i] = codes
             h_planes[i] = planes
-            gate_in[i] = wide.tile([P, D], F32, name="gate_in")
 
-        def add_bias(i, j):
-            cols = slice(SLICE * j, SLICE * (j + 1))
-            nc.gpsimd.tensor_tensor(
-                out=gate_in[i][:, cols], in0=x2g_sb[i][:, cols], in1=bias_all[:, cols], op=ADD
-            )
+        def cols_of(j):
+            return slice(SLICE * j, SLICE * (j + 1))
 
-        def one_slice(i, j, blended):
-            cols = slice(SLICE * j, SLICE * (j + 1))
+        def role_product(i, j):
             hh = psum.tile([P, SLICE], F32, tag="hh", bufs=3)
-            nc.tensor.matmul(hh[:], lhsT=roles_t[i][:, j, :], rhs=vr_sb[:, cols], start=True, stop=True)
-            logits = psum.tile([P, SLICE], F32, tag="acc", bufs=3)
+            hh_of[i, j] = hh
+            alone = j in vector_side(i)
+            nc.tensor.matmul(hh[:], lhsT=roles_t[i][:, j, :], rhs=vr_sb[:, cols_of(j)], start=True, stop=alone)
+            if not alone:
+                nc.tensor.matmul(hh[:], lhsT=minus_ident[:], rhs=h_sb[i][:, cols_of(j)], start=False, stop=True)
+
+        def logits(i, j):
+            acc = psum.tile([P, SLICE], F32, tag="acc", bufs=3)
+            acc_of[i, j] = acc
             for g in range(PASSES):
                 rows_g = slice(P * g, P * (g + 1))
                 nc.tensor.matmul_mx(
-                    out=logits[:],
+                    out=acc[:],
                     lhsT=h_codes[i][:, rows_g].bitcast(FP8X4),
                     lhsT_scale=h_planes[i][:, rows_g],
                     rhs=w_words[:, g, 2 * SLICE * j : 2 * SLICE * (j + 1)].bitcast(FP4X4),
-                    rhs_scale=w_planes[:, g, cols],
+                    rhs_scale=w_planes[:, g, cols_of(j)],
                     start=(g == 0),
                     stop=(g == PASSES - 1),
                 )
-            z = work.tile([P, SLICE], F32)
-            nc.vector.tensor_tensor(out=z[:], in0=logits[:], in1=gate_in[i][:, cols], op=ADD)
-            keep = work.tile([P, SLICE], F32)
-            nc.scalar.activation(out=keep[:], in_=z[:], func=ACT.Sigmoid, scale=-1.0)
-            diff = work.tile([P, SLICE], F32)
-            nc.vector.tensor_tensor(out=diff[:], in0=hh[:], in1=h_sb[i][:, cols], op=SUBTRACT)
-            back = work.tile([P, SLICE], F32)
-            multiplier = nc.vector if j == S - 1 else nc.gpsimd
-            multiplier.tensor_tensor(out=back[:], in0=keep[:], in1=diff[:], op=MULT)
-            nc.vector.tensor_tensor(out=blended[:, cols], in0=hh[:], in1=back[:], op=SUBTRACT)
 
-        transpose_and_quantise(0)
+        def gate_value(i, j):
+            g_cols = gate[i][:, cols_of(j)]
+            nc.vector.tensor_tensor(out=g_cols, in0=acc_of[i, j][:], in1=g_cols, op=ADD)
+            nc.scalar.activation(out=g_cols, in_=g_cols, func=ACT.Sigmoid)
+
+        def subtract_on_vector(i, j):
+            diff = work.tile([P, SLICE], F32, name="diff")
+            diff_sb[i, j] = diff
+            nc.vector.tensor_tensor(out=diff[:], in0=hh_of[i, j][:], in1=h_sb[i][:, cols_of(j)], op=SUBTRACT)
+
+        def product(i, j):
+            g_cols = gate[i][:, cols_of(j)]
+            factor = diff_sb[i, j] if j in vector_side(i) else hh_of[i, j]
+            nc.vector.tensor_tensor(out=g_cols, in0=factor[:], in1=g_cols, op=MULT)
+
+        transpose_h(0)
+        transpose_a(0)
+        quantise(0)
+        gate[0] = gates.tile([P, D], F32, name="gate")
         for j in range(S):
-            add_bias(0, j)
+            nc.vector.tensor_tensor(
+                out=gate[0][:, cols_of(j)], in0=x2g_sb[0][:, cols_of(j)], in1=bias_all[:, cols_of(j)], op=ADD
+            )
+        transpose_h(1)
+        transpose_a(1)
+        quantise(1)
+
         for i in range(ROW_TILES):
-            if i + 1 < ROW_TILES:
-                transpose_and_quantise(i + 1)
-            blended = wide.tile([P, D], F32)
+            last = i == ROW_TILES - 1
+            ahead = i + 2 if i + 2 < ROW_TILES else None
+            if not last:
+                gate[i + 1] = gates.tile([P, D], F32, name="gate")
+                nc.gpsimd.tensor_tensor(out=gate[i + 1][:], in0=x2g_sb[i + 1][:], in1=bias_all[:], op=ADD)
+            side = vector_side(i)
+            if ahead is not None:
+                transpose_h(ahead)
+            for j in side:
+                role_product(i, j)
+            if ahead is not None:
+                transpose_a(ahead)
+            blended = outs.tile([P, D], F32, name="blended")
+
+            def finish(j):
+                product(i, j)
+                if last:
+                    nc.vector.tensor_tensor(
+                        out=blended[:, cols_of(j)], in0=gate[i][:, cols_of(j)], in1=h_sb[i][:, cols_of(j)], op=ADD
+                    )
+                    nc.sync.dma_start(out=out_rows[i][:, cols_of(j)], in_=blended[:, cols_of(j)])
+
             for j in range(S):
-                one_slice(i, j, blended)
-                if i + 1 < ROW_TILES:
-                    add_bias(i + 1, j)
-            nc.sync.dma_start(out=out_rows[i], in_=blended[:])
+                logits(i, j)
+                if j not in side:
+                    role_product(i, j)
+                gate_value(i, j)
+                if j < len(side):
+                    subtract_on_vector(i, side[j])
+                if j >= 1 and j - 1 not in side:
+                    finish(j - 1)
+            if ahead is not None:
+                quantise(ahead)
+            for j in side:
+                finish(j)
+            if not last:
+                nc.vector.tensor_tensor(out=blended[:], in0=gate[i][:], in1=h_sb[i][:], op=ADD)
+                nc.sync.dma_start(out=out_rows[i], in_=blended[:])

@@ -46,15 +46,19 @@ def tile_tpru_pb_kernel(tc, a, vr, h, x2g, w_g_words, w_g_scales, b_g, bg, out):
         psum = ctx.enter_context(tc.psum_pool(name="psum", bufs=2))
         ctx.enter_context(tc.manual_schedule())
 
-        w_planes = const.tile([P, PASSES, D], U8, align_bytes=64)
-        nc.vector.memset(w_planes[:].rearrange("p g n -> p (g n)").bitcast(I32), 0)
-        bias_row = const.tile([P, D], BF16)
-        nc.gpsimd.memset(bias_row[:], 0.0)
-        ones = const.tile([P, P], BF16)
-        nc.gpsimd.memset(ones[:], 1.0)
         warm = const.tile([P, 2], F32)
         nc.vector.memset(warm[:], 0.0)
         nc.scalar.activation(out=warm[:, 1:2], in_=warm[:, 0:1], func=ACT.Sigmoid)
+        bias_row = const.tile([P, D], BF16)
+        nc.vector.memset(bias_row[:], 0.0)
+        w_planes = const.tile([P, PASSES, D], U8, align_bytes=64)
+        nc.vector.memset(w_planes[:].rearrange("p g n -> p (g n)").bitcast(I32), 0)
+        ident = const.tile([P, P], F32)
+        make_identity(nc, ident[:])
+        ones = const.tile([P, P], BF16)
+        nc.gpsimd.memset(ones[:], 1.0)
+        ident_bf16 = const.tile([P, P], BF16)
+        make_identity(nc, ident_bf16[:])
 
         h_sb, x2g_sb, a_sb = {}, {}, {}
 
@@ -68,17 +72,6 @@ def tile_tpru_pb_kernel(tc, a, vr, h, x2g, w_g_words, w_g_scales, b_g, bg, out):
             x2g_sb[i] = rows.tile([P, D], BF16, name="x2g_tile")
             nc.sync.dma_start(out=x2g_sb[i][:], in_=x2g_rows[i])
 
-        load_h_a(0)
-        nc.sync.dma_start(out=bias_row[0:1, :], in_=b_g.unsqueeze(0))
-        bg_bf16 = const.tile([P, 1], BF16)
-        nc.sync.dma_start(out=bg_bf16[:], in_=bg.partition_broadcast(P))
-        scales_by_row = w_g_scales.rearrange("g q n -> q g n")
-        for first in range(8):
-            partition = 32 * (first // 4) + first % 4
-            nc.sync.dma_start(
-                out=w_planes[partition:P:64, :, :].bitcast(I32),
-                in_=scales_by_row[first:16:8].bitcast(I32),
-            )
         w_words = const.tile([P, PASSES, 2 * D], U8, align_bytes=64)
         words_by_partition = w_g_words.rearrange("g p c -> p g c")
         vr_sb = const.tile([P, D], BF16)
@@ -90,35 +83,36 @@ def tile_tpru_pb_kernel(tc, a, vr, h, x2g, w_g_words, w_g_scales, b_g, bg, out):
                 in_=words_by_partition[:, :, word_cols].bitcast(I32),
             )
 
+        load_h_a(0)
         load_w(0)
-        nc.sync.dma_start(out=vr_sb[:], in_=vr.rearrange("n s d -> n (s d)"))
-        load_h_a(1)
+        nc.sync.dma_start(out=bias_row[0:1, :], in_=b_g.unsqueeze(0))
+        bg_bf16 = const.tile([P, 1], BF16)
+        nc.sync.dma_start(out=bg_bf16[:], in_=bg.partition_broadcast(P))
+        scales_by_row = w_g_scales.rearrange("g q n -> q g n")
+        for r in range(4):
+            nc.sync.dma_start(
+                out=w_planes[r:P:32, :, :].bitcast(I32),
+                in_=scales_by_row[r:16:4].bitcast(I32),
+            )
         load_x2g(0)
+        nc.sync.dma_start(out=vr_sb[:], in_=vr.rearrange("n s d -> n (s d)"))
         load_x2g(1)
+        load_h_a(1)
         load_w(1)
         load_w(2)
+        load_h_a(2)
         load_w(3)
-        for i in range(2, ROW_TILES):
+        load_x2g(2)
+        for i in range(3, ROW_TILES):
             load_h_a(i)
             load_x2g(i)
 
-        ident = const.tile([P, P], F32)
-        make_identity(nc, ident[:])
-        ident_bf16 = const.tile([P, P], BF16)
-        make_identity(nc, ident_bf16[:])
         minus_ident = const.tile([P, P], BF16)
         nc.vector.tensor_scalar_mul(out=minus_ident[:], in0=ident_bf16[:], scalar1=-1.0)
         bg_f32 = const.tile([P, 1], F32)
         nc.vector.tensor_copy(out=bg_f32[:], in_=bg_bf16[:])
 
         bias_all = const.tile([P, D], F32)
-        for j in range(S):
-            cols = slice(SLICE * j, SLICE * (j + 1))
-            spread = psum.tile([P, SLICE], F32, tag="acc", bufs=3)
-            nc.tensor.matmul(spread[:], lhsT=ones[:], rhs=bias_row[:, cols], start=True, stop=True)
-            nc.scalar.activation(
-                out=bias_all[:, cols], in_=spread[:], func=ACT.Identity, bias=bg_f32[:, 0:1], scale=1.0
-            )
 
         h_codes, h_planes, roles_t, grouped_of, gate, hh_of, acc_of, diff_sb = {}, {}, {}, {}, {}, {}, {}, {}
 
@@ -128,7 +122,7 @@ def tile_tpru_pb_kernel(tc, a, vr, h, x2g, w_g_words, w_g_scales, b_g, bg, out):
             grouped_of[i] = grouped
             grouped_words = grouped[:].bitcast(F32).rearrange("p (g b u) -> p g b u", g=PASSES, b=P, u=2)
             for half in range(2):
-                flipped = psum.tile([P, 2, 2, P], F32, tag="tr", bufs=2)
+                flipped = psum.tile([P, 2, 2, P], F32, tag="tr", bufs=3)
                 for gg in range(2):
                     g = 2 * half + gg
                     for u in range(2):
@@ -142,7 +136,7 @@ def tile_tpru_pb_kernel(tc, a, vr, h, x2g, w_g_words, w_g_scales, b_g, bg, out):
 
         def transpose_a(i):
             a_words = a_sb[i][:].bitcast(F32)
-            a_flipped = psum.tile([P, 2, P], F32, tag="tr", bufs=2)
+            a_flipped = psum.tile([P, 2, P], F32, tag="tr", bufs=3)
             for u in range(2):
                 nc.tensor.transpose(a_flipped[:, u, :], a_words[:, u : 2 * ROLES : 2], ident[:])
             a_t = prep.tile([P, S, P], BF16, name="a_t")
@@ -174,7 +168,7 @@ def tile_tpru_pb_kernel(tc, a, vr, h, x2g, w_g_words, w_g_scales, b_g, bg, out):
                 nc.tensor.matmul(hh[:], lhsT=minus_ident[:], rhs=h_sb[i][:, cols_of(j)], start=False, stop=True)
 
         def logits(i, j):
-            acc = psum.tile([P, SLICE], F32, tag="acc", bufs=3)
+            acc = psum.tile([P, SLICE], F32, tag="acc", bufs=2)
             acc_of[i, j] = acc
             for g in range(PASSES):
                 rows_g = slice(P * g, P * (g + 1))
@@ -203,54 +197,99 @@ def tile_tpru_pb_kernel(tc, a, vr, h, x2g, w_g_words, w_g_scales, b_g, bg, out):
             factor = diff_sb[i, j] if j in vector_side(i) else hh_of[i, j]
             nc.vector.tensor_tensor(out=g_cols, in0=factor[:], in1=g_cols, op=MULT)
 
+        def final_add(i, j, blended):
+            nc.vector.tensor_tensor(
+                out=blended[:, cols_of(j)], in0=gate[i][:, cols_of(j)], in1=h_sb[i][:, cols_of(j)], op=ADD
+            )
+            nc.sync.dma_start(out=out_rows[i][:, cols_of(j)], in_=blended[:, cols_of(j)])
+
+        def start_gate(i):
+            gate[i] = gates.tile([P, D], F32, name="gate")
+            nc.gpsimd.tensor_tensor(out=gate[i][:], in0=x2g_sb[i][:], in1=bias_all[:], op=ADD)
+
         transpose_h(0)
         transpose_a(0)
+        spread_of = {}
+        for j in range(S):
+            if j < 2:
+                spread = psum.tile([P, SLICE], F32, tag="acc", bufs=2)
+            else:
+                spread = psum.tile([P, SLICE], F32, tag="hh", bufs=3)
+            spread_of[j] = spread
+            nc.tensor.matmul(spread[:], lhsT=ones[:], rhs=bias_row[:, cols_of(j)], start=True, stop=True)
+            nc.scalar.activation(
+                out=bias_all[:, cols_of(j)], in_=spread[:], func=ACT.Identity, bias=bg_f32[:, 0:1], scale=1.0
+            )
         quantise(0)
         gate[0] = gates.tile([P, D], F32, name="gate")
         for j in range(S):
-            nc.vector.tensor_tensor(
-                out=gate[0][:, cols_of(j)], in0=x2g_sb[0][:, cols_of(j)], in1=bias_all[:, cols_of(j)], op=ADD
+            nc.vector.scalar_tensor_tensor(
+                out=gate[0][:, cols_of(j)],
+                in0=spread_of[j][:],
+                scalar=bg_f32[:, 0:1],
+                in1=x2g_sb[0][:, cols_of(j)],
+                op0=ADD,
+                op1=ADD,
             )
+        start_gate(1)
+
+        blended = outs.tile([P, D], F32, name="blended")
+        logits(0, 0)
+        gate_value(0, 0)
+        role_product(0, 3)
+        role_product(0, 2)
+        role_product(0, 0)
+        subtract_on_vector(0, 3)
+        subtract_on_vector(0, 2)
         transpose_h(1)
         transpose_a(1)
+        logits(0, 1)
+        role_product(0, 1)
+        gate_value(0, 1)
         quantise(1)
+        product(0, 0)
+        final_add(0, 0, blended)
+        logits(0, 2)
+        gate_value(0, 2)
+        product(0, 1)
+        final_add(0, 1, blended)
+        transpose_h(2)
+        transpose_a(2)
+        logits(0, 3)
+        gate_value(0, 3)
+        quantise(2)
+        product(0, 2)
+        final_add(0, 2, blended)
+        product(0, 3)
+        final_add(0, 3, blended)
 
-        for i in range(ROW_TILES):
+        for i in range(1, ROW_TILES):
             last = i == ROW_TILES - 1
             ahead = i + 2 if i + 2 < ROW_TILES else None
             if not last:
-                gate[i + 1] = gates.tile([P, D], F32, name="gate")
-                nc.gpsimd.tensor_tensor(out=gate[i + 1][:], in0=x2g_sb[i + 1][:], in1=bias_all[:], op=ADD)
-            side = vector_side(i)
+                start_gate(i + 1)
             if ahead is not None:
                 transpose_h(ahead)
-            for j in side:
-                role_product(i, j)
+            role_product(i, 3)
             if ahead is not None:
                 transpose_a(ahead)
             blended = outs.tile([P, D], F32, name="blended")
-
-            def finish(j):
-                product(i, j)
-                if last:
-                    nc.vector.tensor_tensor(
-                        out=blended[:, cols_of(j)], in0=gate[i][:, cols_of(j)], in1=h_sb[i][:, cols_of(j)], op=ADD
-                    )
-                    nc.sync.dma_start(out=out_rows[i][:, cols_of(j)], in_=blended[:, cols_of(j)])
-
             for j in range(S):
                 logits(i, j)
-                if j not in side:
+                if j < 3:
                     role_product(i, j)
                 gate_value(i, j)
-                if j < len(side):
-                    subtract_on_vector(i, side[j])
-                if j >= 1 and j - 1 not in side:
-                    finish(j - 1)
+                if j == 0:
+                    subtract_on_vector(i, 3)
+                else:
+                    product(i, j - 1)
+                    if last:
+                        final_add(i, j - 1, blended)
             if ahead is not None:
                 quantise(ahead)
-            for j in side:
-                finish(j)
-            if not last:
+            product(i, 3)
+            if last:
+                final_add(i, 3, blended)
+            else:
                 nc.vector.tensor_tensor(out=blended[:], in0=gate[i][:], in1=h_sb[i][:], op=ADD)
                 nc.sync.dma_start(out=out_rows[i], in_=blended[:])

@@ -49,10 +49,10 @@ def tile_tpru_pb_kernel(tc, a, vr, h, x2g, w_g_words, w_g_scales, b_g, bg, out):
         warm = const.tile([P, 2], F32)
         nc.vector.memset(warm[:], 0.0)
         nc.scalar.activation(out=warm[:, 1:2], in_=warm[:, 0:1], func=ACT.Sigmoid)
-        bias_row = const.tile([P, D], BF16)
-        nc.vector.memset(bias_row[:], 0.0)
         w_planes = const.tile([P, PASSES, D], U8, align_bytes=64)
         nc.vector.memset(w_planes[:].rearrange("p g n -> p (g n)").bitcast(I32), 0)
+        bias_row = const.tile([P, D], BF16)
+        nc.gpsimd.memset(bias_row[:], 0.0)
         ident = const.tile([P, P], F32)
         make_identity(nc, ident[:])
         ones = const.tile([P, P], BF16)
@@ -72,19 +72,20 @@ def tile_tpru_pb_kernel(tc, a, vr, h, x2g, w_g_words, w_g_scales, b_g, bg, out):
             x2g_sb[i] = rows.tile([P, D], BF16, name="x2g_tile")
             nc.sync.dma_start(out=x2g_sb[i][:], in_=x2g_rows[i])
 
-        w_words = const.tile([P, PASSES, 2 * D], U8, align_bytes=64)
+        w_words = {}
         words_by_partition = w_g_words.rearrange("g p c -> p g c")
         vr_sb = const.tile([P, D], BF16)
 
         def load_w(j):
-            word_cols = slice(2 * SLICE * j, 2 * SLICE * (j + 1))
+            w_words[j] = const.tile([P, PASSES, 2 * SLICE], U8, align_bytes=64, name="w_words_%d" % j)
             nc.sync.dma_start(
-                out=w_words[:, :, word_cols].bitcast(I32),
-                in_=words_by_partition[:, :, word_cols].bitcast(I32),
+                out=w_words[j][:].bitcast(I32),
+                in_=words_by_partition[:, :, 2 * SLICE * j : 2 * SLICE * (j + 1)].bitcast(I32),
             )
 
         load_h_a(0)
         load_w(0)
+        load_x2g(0)
         nc.sync.dma_start(out=bias_row[0:1, :], in_=b_g.unsqueeze(0))
         bg_bf16 = const.tile([P, 1], BF16)
         nc.sync.dma_start(out=bg_bf16[:], in_=bg.partition_broadcast(P))
@@ -94,7 +95,6 @@ def tile_tpru_pb_kernel(tc, a, vr, h, x2g, w_g_words, w_g_scales, b_g, bg, out):
                 out=w_planes[r:P:32, :, :].bitcast(I32),
                 in_=scales_by_row[r:16:4].bitcast(I32),
             )
-        load_x2g(0)
         nc.sync.dma_start(out=vr_sb[:], in_=vr.rearrange("n s d -> n (s d)"))
         load_x2g(1)
         load_h_a(1)
@@ -176,7 +176,7 @@ def tile_tpru_pb_kernel(tc, a, vr, h, x2g, w_g_words, w_g_scales, b_g, bg, out):
                     out=acc[:],
                     lhsT=h_codes[i][:, rows_g].bitcast(FP8X4),
                     lhsT_scale=h_planes[i][:, rows_g],
-                    rhs=w_words[:, g, 2 * SLICE * j : 2 * SLICE * (j + 1)].bitcast(FP4X4),
+                    rhs=w_words[j][:, g, :].bitcast(FP4X4),
                     rhs_scale=w_planes[:, g, cols_of(j)],
                     start=(g == 0),
                     stop=(g == PASSES - 1),
@@ -211,10 +211,10 @@ def tile_tpru_pb_kernel(tc, a, vr, h, x2g, w_g_words, w_g_scales, b_g, bg, out):
         transpose_a(0)
         spread_of = {}
         for j in range(S):
-            if j < 2:
-                spread = psum.tile([P, SLICE], F32, tag="acc", bufs=2)
-            else:
+            if j < 3:
                 spread = psum.tile([P, SLICE], F32, tag="hh", bufs=3)
+            else:
+                spread = psum.tile([P, SLICE], F32, tag="acc", bufs=2)
             spread_of[j] = spread
             nc.tensor.matmul(spread[:], lhsT=ones[:], rhs=bias_row[:, cols_of(j)], start=True, stop=True)
             nc.scalar.activation(

@@ -185,7 +185,7 @@ def tile_tpru_pb_kernel(tc, a, vr, h, x2g, w_g_words, w_g_scales, b_g, bg, out):
         def gate_value(i, j):
             g_cols = gate[i][:, cols_of(j)]
             nc.vector.tensor_tensor(out=g_cols, in0=acc_of[i, j][:], in1=g_cols, op=ADD)
-            nc.scalar.activation(out=g_cols, in_=g_cols, func=ACT.Sigmoid)
+            nc.scalar.activation(out=g_cols, in_=g_cols, func=ACT.Sigmoid, scale=-1.0 if j in vector_side(i) else 1.0)
 
         def subtract_on_vector(i, j):
             diff = work.tile([P, SLICE], F32, name="diff")
@@ -194,8 +194,14 @@ def tile_tpru_pb_kernel(tc, a, vr, h, x2g, w_g_words, w_g_scales, b_g, bg, out):
 
         def product(i, j):
             g_cols = gate[i][:, cols_of(j)]
-            factor = diff_sb[i, j] if j in vector_side(i) else hh_of[i, j]
-            nc.vector.tensor_tensor(out=g_cols, in0=factor[:], in1=g_cols, op=MULT)
+            nc.vector.tensor_tensor(out=g_cols, in0=hh_of[i, j][:], in1=g_cols, op=MULT)
+
+        def hold_back(i, j):
+            diff = diff_sb[i, j]
+            nc.vector.tensor_tensor(out=diff[:], in0=diff[:], in1=gate[i][:, cols_of(j)], op=MULT)
+
+        def from_roles(i, j, blended):
+            nc.vector.tensor_tensor(out=blended[:, cols_of(j)], in0=hh_of[i, j][:], in1=diff_sb[i, j][:], op=SUBTRACT)
 
         def final_add(i, j, blended):
             nc.vector.tensor_tensor(
@@ -233,14 +239,11 @@ def tile_tpru_pb_kernel(tc, a, vr, h, x2g, w_g_words, w_g_scales, b_g, bg, out):
             )
         start_gate(1)
 
-        blended = outs.tile([P, D], F32, name="blended")
+        blended_of = {}
+        blended_of[0] = outs.tile([P, D], F32, name="blended")
         logits(0, 0)
         gate_value(0, 0)
-        role_product(0, 3)
-        role_product(0, 2)
         role_product(0, 0)
-        subtract_on_vector(0, 3)
-        subtract_on_vector(0, 2)
         transpose_h(1)
         transpose_a(1)
         logits(0, 1)
@@ -248,20 +251,28 @@ def tile_tpru_pb_kernel(tc, a, vr, h, x2g, w_g_words, w_g_scales, b_g, bg, out):
         gate_value(0, 1)
         quantise(1)
         product(0, 0)
-        final_add(0, 0, blended)
+        final_add(0, 0, blended_of[0])
         logits(0, 2)
+        role_product(0, 2)
         gate_value(0, 2)
         product(0, 1)
-        final_add(0, 1, blended)
+        final_add(0, 1, blended_of[0])
+        subtract_on_vector(0, 2)
         transpose_h(2)
         transpose_a(2)
         logits(0, 3)
+        role_product(0, 3)
         gate_value(0, 3)
+        subtract_on_vector(0, 3)
         quantise(2)
-        product(0, 2)
-        final_add(0, 2, blended)
-        product(0, 3)
-        final_add(0, 3, blended)
+        hold_back(0, 2)
+        hold_back(0, 3)
+
+        def finish_vector_side(i):
+            first = vector_side(i)[0]
+            for j in vector_side(i):
+                from_roles(i, j, blended_of[i])
+            nc.sync.dma_start(out=out_rows[i][:, SLICE * first :], in_=blended_of[i][:, SLICE * first :])
 
         for i in range(1, ROW_TILES):
             last = i == ROW_TILES - 1
@@ -270,26 +281,26 @@ def tile_tpru_pb_kernel(tc, a, vr, h, x2g, w_g_words, w_g_scales, b_g, bg, out):
                 start_gate(i + 1)
             if ahead is not None:
                 transpose_h(ahead)
-            role_product(i, 3)
-            if ahead is not None:
                 transpose_a(ahead)
-            blended = outs.tile([P, D], F32, name="blended")
+            blended_of[i] = outs.tile([P, D], F32, name="blended")
             for j in range(S):
                 logits(i, j)
-                if j < 3:
-                    role_product(i, j)
+                role_product(i, j)
                 gate_value(i, j)
                 if j == 0:
-                    subtract_on_vector(i, 3)
+                    finish_vector_side(i - 1)
                 else:
                     product(i, j - 1)
                     if last:
-                        final_add(i, j - 1, blended)
+                        final_add(i, j - 1, blended_of[i])
+            subtract_on_vector(i, 3)
             if ahead is not None:
                 quantise(ahead)
-            product(i, 3)
-            if last:
-                final_add(i, 3, blended)
-            else:
-                nc.vector.tensor_tensor(out=blended[:], in0=gate[i][:], in1=h_sb[i][:], op=ADD)
-                nc.sync.dma_start(out=out_rows[i], in_=blended[:])
+            hold_back(i, 3)
+            if not last:
+                tensor_cols = slice(0, 3 * SLICE)
+                nc.vector.tensor_tensor(
+                    out=blended_of[i][:, tensor_cols], in0=gate[i][:, tensor_cols], in1=h_sb[i][:, tensor_cols], op=ADD
+                )
+                nc.sync.dma_start(out=out_rows[i][:, tensor_cols], in_=blended_of[i][:, tensor_cols])
+        finish_vector_side(ROW_TILES - 1)

@@ -203,8 +203,8 @@ def tile_tpru_pb_kernel(tc, a, vr, h, x2g, w_g_words, w_g_scales, b_g, bg, out):
         def from_roles(i, j, blended):
             nc.vector.tensor_tensor(out=blended[:, cols_of(j)], in0=hh_of[i, j][:], in1=diff_sb[i, j][:], op=SUBTRACT)
 
-        def final_add(i, j, blended):
-            nc.vector.tensor_tensor(
+        def final_add(i, j, blended, engine):
+            engine.tensor_tensor(
                 out=blended[:, cols_of(j)], in0=gate[i][:, cols_of(j)], in1=h_sb[i][:, cols_of(j)], op=ADD
             )
             nc.sync.dma_start(out=out_rows[i][:, cols_of(j)], in_=blended[:, cols_of(j)])
@@ -251,12 +251,12 @@ def tile_tpru_pb_kernel(tc, a, vr, h, x2g, w_g_words, w_g_scales, b_g, bg, out):
         gate_value(0, 1)
         quantise(1)
         product(0, 0)
-        final_add(0, 0, blended_of[0])
+        final_add(0, 0, blended_of[0], nc.gpsimd)
         logits(0, 2)
         role_product(0, 2)
         gate_value(0, 2)
         product(0, 1)
-        final_add(0, 1, blended_of[0])
+        final_add(0, 1, blended_of[0], nc.gpsimd)
         subtract_on_vector(0, 2)
         transpose_h(2)
         transpose_a(2)
@@ -292,7 +292,7 @@ def tile_tpru_pb_kernel(tc, a, vr, h, x2g, w_g_words, w_g_scales, b_g, bg, out):
                 else:
                     product(i, j - 1)
                     if last:
-                        final_add(i, j - 1, blended_of[i])
+                        final_add(i, j - 1, blended_of[i], nc.gpsimd if j < 3 else nc.vector)
             subtract_on_vector(i, 3)
             if ahead is not None:
                 quantise(ahead)

@@ -21,12 +21,13 @@ SLICE = D // S
 K_PASS = 4 * P
 PASSES = D // K_PASS
 ROW_TILES = B // P
+TR_BANKS, ACC_BANKS, HH_BANKS = 3, 3, 2
 
 FLOPS = 2 * B * D * D + 2 * B * ROLES * D
 
 
 def vector_side(i):
-    return (2, 3) if i == 0 else (3,)
+    return (0, 1) if i == 0 else (0,)
 
 
 def tile_tpru_pb_kernel(tc, a, vr, h, x2g, w_g_words, w_g_scales, b_g, bg, out):
@@ -35,6 +36,7 @@ def tile_tpru_pb_kernel(tc, a, vr, h, x2g, w_g_words, w_g_scales, b_g, bg, out):
     x2g_rows = x2g.rearrange("(i p) d -> i p d", p=P)
     a_rows = a.rearrange("(i p) n s -> i p (n s)", p=P)
     out_rows = out.rearrange("(i p) d -> i p d", p=P)
+    vr_rows = vr.rearrange("n s d -> n (s d)")
 
     with ExitStack() as ctx:
         const = ctx.enter_context(tc.tile_pool(name="const", bufs=1))
@@ -49,10 +51,10 @@ def tile_tpru_pb_kernel(tc, a, vr, h, x2g, w_g_words, w_g_scales, b_g, bg, out):
         warm = const.tile([P, 2], F32)
         nc.vector.memset(warm[:], 0.0)
         nc.scalar.activation(out=warm[:, 1:2], in_=warm[:, 0:1], func=ACT.Sigmoid)
+        bias_row = const.tile([P, D], BF16)
+        nc.vector.memset(bias_row[:].bitcast(I32), 0)
         w_planes = const.tile([P, PASSES, D], U8, align_bytes=64)
         nc.vector.memset(w_planes[:].rearrange("p g n -> p (g n)").bitcast(I32), 0)
-        bias_row = const.tile([P, D], BF16)
-        nc.gpsimd.memset(bias_row[:], 0.0)
         ident = const.tile([P, P], F32)
         make_identity(nc, ident[:])
         ones = const.tile([P, P], BF16)
@@ -62,19 +64,26 @@ def tile_tpru_pb_kernel(tc, a, vr, h, x2g, w_g_words, w_g_scales, b_g, bg, out):
 
         h_sb, x2g_sb, a_sb = {}, {}, {}
 
-        def load_h_a(i):
+        def load_h(i):
             h_sb[i] = rows.tile([P, D], BF16, name="h_tile")
             nc.sync.dma_start(out=h_sb[i][:], in_=h_rows[i])
+
+        def load_a(i):
             a_sb[i] = rows.tile([P, ROLES * S], BF16, name="a_tile")
             nc.sync.dma_start(out=a_sb[i][:], in_=a_rows[i])
 
-        def load_x2g(i):
-            x2g_sb[i] = rows.tile([P, D], BF16, name="x2g_tile")
-            nc.sync.dma_start(out=x2g_sb[i][:], in_=x2g_rows[i])
+        def load_x2g(i, cols=slice(0, D)):
+            if i not in x2g_sb:
+                x2g_sb[i] = rows.tile([P, D], BF16, name="x2g_tile")
+            nc.sync.dma_start(out=x2g_sb[i][:, cols], in_=x2g_rows[i][:, cols])
+
+        vr_sb = const.tile([P, D], BF16)
+
+        def load_vr(cols):
+            nc.sync.dma_start(out=vr_sb[:, cols], in_=vr_rows[:, cols])
 
         w_words = {}
         words_by_partition = w_g_words.rearrange("g p c -> p g c")
-        vr_sb = const.tile([P, D], BF16)
 
         def load_w(j):
             w_words[j] = const.tile([P, PASSES, 2 * SLICE], U8, align_bytes=64, name="w_words_%d" % j)
@@ -83,9 +92,9 @@ def tile_tpru_pb_kernel(tc, a, vr, h, x2g, w_g_words, w_g_scales, b_g, bg, out):
                 in_=words_by_partition[:, :, 2 * SLICE * j : 2 * SLICE * (j + 1)].bitcast(I32),
             )
 
-        load_h_a(0)
+        load_h(0)
+        load_a(0)
         load_w(0)
-        load_x2g(0)
         nc.sync.dma_start(out=bias_row[0:1, :], in_=b_g.unsqueeze(0))
         bg_bf16 = const.tile([P, 1], BF16)
         nc.sync.dma_start(out=bg_bf16[:], in_=bg.partition_broadcast(P))
@@ -95,16 +104,18 @@ def tile_tpru_pb_kernel(tc, a, vr, h, x2g, w_g_words, w_g_scales, b_g, bg, out):
                 out=w_planes[r:P:32, :, :].bitcast(I32),
                 in_=scales_by_row[r:16:4].bitcast(I32),
             )
-        nc.sync.dma_start(out=vr_sb[:], in_=vr.rearrange("n s d -> n (s d)"))
+        for j in range(S):
+            if j > 0:
+                load_w(j)
+            if j == 2:
+                load_h(1)
+            load_x2g(0, slice(SLICE * j, SLICE * (j + 1)))
+            load_vr(slice(SLICE * j, SLICE * (j + 1)))
+        load_a(1)
         load_x2g(1)
-        load_h_a(1)
-        load_w(1)
-        load_w(2)
-        load_h_a(2)
-        load_w(3)
-        load_x2g(2)
-        for i in range(3, ROW_TILES):
-            load_h_a(i)
+        for i in range(2, ROW_TILES):
+            load_h(i)
+            load_a(i)
             load_x2g(i)
 
         minus_ident = const.tile([P, P], BF16)
@@ -116,29 +127,48 @@ def tile_tpru_pb_kernel(tc, a, vr, h, x2g, w_g_words, w_g_scales, b_g, bg, out):
 
         h_codes, h_planes, roles_t, grouped_of, gate, hh_of, acc_of, diff_sb = {}, {}, {}, {}, {}, {}, {}, {}
 
+        h_apart, a_apart = {}, {}
+
+        def part_h(i, half):
+            if i not in h_apart:
+                h_apart[i] = prep.tile([P, D], BF16, name="h_apart")
+            words = slice(D // 4 * half, D // 4 * (half + 1))
+            nc.scalar.copy(
+                out=h_apart[i][:].bitcast(F32)[:, words].rearrange("p (g u w) -> p g u w", u=2, w=P),
+                in_=h_sb[i][:].bitcast(F32)[:, words].rearrange("p (g w u) -> p g u w", u=2, w=P),
+            )
+
+        def part_a(i):
+            a_apart[i] = prep.tile([P, ROLES * S], BF16, name="a_apart")
+            nc.scalar.copy(
+                out=a_apart[i][:].bitcast(F32).rearrange("p (u n) -> p u n", u=2),
+                in_=a_sb[i][:].bitcast(F32).rearrange("p (n u) -> p u n", u=2),
+            )
+
+        def words_of(source, apart, i, start, u):
+            if i in apart:
+                return apart[i][:].bitcast(F32)[:, start + P * u : start + P * (u + 1)]
+            return source[i][:].bitcast(F32)[:, start + u : start + 2 * P : 2]
+
         def transpose_h(i):
-            h_words = h_sb[i][:].bitcast(F32)
             grouped = prep.tile([P, D], BF16, align_bytes=64, name="grouped")
             grouped_of[i] = grouped
             grouped_words = grouped[:].bitcast(F32).rearrange("p (g b u) -> p g b u", g=PASSES, b=P, u=2)
             for half in range(2):
-                flipped = psum.tile([P, 2, 2, P], F32, tag="tr", bufs=3)
+                flipped = psum.tile([P, 2, 2, P], F32, tag="tr", bufs=TR_BANKS)
                 for gg in range(2):
                     g = 2 * half + gg
                     for u in range(2):
-                        nc.tensor.transpose(
-                            flipped[:, gg, u, :], h_words[:, 256 * g + u : 256 * (g + 1) : 2], ident[:]
-                        )
+                        nc.tensor.transpose(flipped[:, gg, u, :], words_of(h_sb, h_apart, i, 2 * P * g, u), ident[:])
                 nc.scalar.copy(
                     out=grouped_words[:, 2 * half : 2 * half + 2, :, :],
                     in_=flipped[:].rearrange("p g u b -> p g b u"),
                 )
 
         def transpose_a(i):
-            a_words = a_sb[i][:].bitcast(F32)
-            a_flipped = psum.tile([P, 2, P], F32, tag="tr", bufs=3)
+            a_flipped = psum.tile([P, 2, P], F32, tag="tr", bufs=TR_BANKS)
             for u in range(2):
-                nc.tensor.transpose(a_flipped[:, u, :], a_words[:, u : 2 * ROLES : 2], ident[:])
+                nc.tensor.transpose(a_flipped[:, u, :], words_of(a_sb, a_apart, i, 0, u), ident[:])
             a_t = prep.tile([P, S, P], BF16, name="a_t")
             nc.scalar.copy(
                 out=a_t[:].rearrange("n (u e) b -> n u e b", u=2),
@@ -160,7 +190,7 @@ def tile_tpru_pb_kernel(tc, a, vr, h, x2g, w_g_words, w_g_scales, b_g, bg, out):
             return slice(SLICE * j, SLICE * (j + 1))
 
         def role_product(i, j):
-            hh = psum.tile([P, SLICE], F32, tag="hh", bufs=3)
+            hh = psum.tile([P, SLICE], F32, tag="hh", bufs=HH_BANKS)
             hh_of[i, j] = hh
             alone = j in vector_side(i)
             nc.tensor.matmul(hh[:], lhsT=roles_t[i][:, j, :], rhs=vr_sb[:, cols_of(j)], start=True, stop=alone)
@@ -168,7 +198,7 @@ def tile_tpru_pb_kernel(tc, a, vr, h, x2g, w_g_words, w_g_scales, b_g, bg, out):
                 nc.tensor.matmul(hh[:], lhsT=minus_ident[:], rhs=h_sb[i][:, cols_of(j)], start=False, stop=True)
 
         def logits(i, j):
-            acc = psum.tile([P, SLICE], F32, tag="acc", bufs=2)
+            acc = psum.tile([P, SLICE], F32, tag="acc", bufs=ACC_BANKS)
             acc_of[i, j] = acc
             for g in range(PASSES):
                 rows_g = slice(P * g, P * (g + 1))
@@ -185,50 +215,63 @@ def tile_tpru_pb_kernel(tc, a, vr, h, x2g, w_g_words, w_g_scales, b_g, bg, out):
         def gate_value(i, j):
             g_cols = gate[i][:, cols_of(j)]
             nc.vector.tensor_tensor(out=g_cols, in0=acc_of[i, j][:], in1=g_cols, op=ADD)
-            nc.scalar.activation(out=g_cols, in_=g_cols, func=ACT.Sigmoid, scale=-1.0 if j in vector_side(i) else 1.0)
+            nc.scalar.activation(out=g_cols, in_=g_cols, func=ACT.Sigmoid, scale=-1.0 if i > 0 and j in vector_side(i) else 1.0)
 
-        def subtract_on_vector(i, j):
-            diff = work.tile([P, SLICE], F32, name="diff")
-            diff_sb[i, j] = diff
-            nc.vector.tensor_tensor(out=diff[:], in0=hh_of[i, j][:], in1=h_sb[i][:, cols_of(j)], op=SUBTRACT)
-
-        def product(i, j):
-            g_cols = gate[i][:, cols_of(j)]
-            nc.vector.tensor_tensor(out=g_cols, in0=hh_of[i, j][:], in1=g_cols, op=MULT)
+        def difference(i, j):
+            if j in vector_side(i):
+                diff = work.tile([P, SLICE], F32, name="diff")
+                diff_sb[i, j] = diff
+                nc.vector.tensor_tensor(out=diff[:], in0=hh_of[i, j][:], in1=h_sb[i][:, cols_of(j)], op=SUBTRACT)
+            else:
+                g_cols = gate[i][:, cols_of(j)]
+                nc.vector.tensor_tensor(out=g_cols, in0=hh_of[i, j][:], in1=g_cols, op=MULT)
 
         def hold_back(i, j):
             diff = diff_sb[i, j]
             nc.vector.tensor_tensor(out=diff[:], in0=diff[:], in1=gate[i][:, cols_of(j)], op=MULT)
 
-        def from_roles(i, j, blended):
-            nc.vector.tensor_tensor(out=blended[:, cols_of(j)], in0=hh_of[i, j][:], in1=diff_sb[i, j][:], op=SUBTRACT)
+        def product_apart(i, j):
+            g_cols = gate[i][:, cols_of(j)]
+            nc.vector.tensor_tensor(out=g_cols, in0=diff_sb[i, j][:], in1=g_cols, op=MULT)
 
-        def final_add(i, j, blended, engine):
-            engine.tensor_tensor(
-                out=blended[:, cols_of(j)], in0=gate[i][:, cols_of(j)], in1=h_sb[i][:, cols_of(j)], op=ADD
+        def from_roles(i, j):
+            nc.vector.tensor_tensor(
+                out=blended_of[i][:, cols_of(j)], in0=hh_of[i, j][:], in1=diff_sb[i, j][:], op=SUBTRACT
             )
-            nc.sync.dma_start(out=out_rows[i][:, cols_of(j)], in_=blended[:, cols_of(j)])
 
-        def start_gate(i):
-            gate[i] = gates.tile([P, D], F32, name="gate")
-            nc.gpsimd.tensor_tensor(out=gate[i][:], in0=x2g_sb[i][:], in1=bias_all[:], op=ADD)
+        def store(i, cols):
+            nc.sync.dma_start(out=out_rows[i][:, cols], in_=blended_of[i][:, cols])
 
-        transpose_h(0)
-        transpose_a(0)
+        def final_add(i, cols, engine):
+            engine.tensor_tensor(out=blended_of[i][:, cols], in0=gate[i][:, cols], in1=h_sb[i][:, cols], op=ADD)
+            store(i, cols)
+
+        def gate_input(i, cols):
+            if i not in gate:
+                gate[i] = gates.tile([P, D], F32, name="gate")
+            nc.gpsimd.tensor_tensor(out=gate[i][:, cols], in0=x2g_sb[i][:, cols], in1=bias_all[:, cols], op=ADD)
+
+        blended_of = {}
+
+        def open_output(i):
+            blended_of[i] = outs.tile([P, D], F32, name="blended")
+
         spread_of = {}
-        for j in range(S):
-            if j < 3:
-                spread = psum.tile([P, SLICE], F32, tag="hh", bufs=3)
+
+        def spread_bias(j):
+            if j < 2:
+                spread = psum.tile([P, SLICE], F32, tag="hh", bufs=HH_BANKS)
             else:
-                spread = psum.tile([P, SLICE], F32, tag="acc", bufs=2)
+                spread = psum.tile([P, SLICE], F32, tag="tr", bufs=TR_BANKS)
             spread_of[j] = spread
             nc.tensor.matmul(spread[:], lhsT=ones[:], rhs=bias_row[:, cols_of(j)], start=True, stop=True)
             nc.scalar.activation(
                 out=bias_all[:, cols_of(j)], in_=spread[:], func=ACT.Identity, bias=bg_f32[:, 0:1], scale=1.0
             )
-        quantise(0)
+
         gate[0] = gates.tile([P, D], F32, name="gate")
-        for j in range(S):
+
+        def first_gate_input(j):
             nc.vector.scalar_tensor_tensor(
                 out=gate[0][:, cols_of(j)],
                 in0=spread_of[j][:],
@@ -237,70 +280,100 @@ def tile_tpru_pb_kernel(tc, a, vr, h, x2g, w_g_words, w_g_scales, b_g, bg, out):
                 op0=ADD,
                 op1=ADD,
             )
-        start_gate(1)
 
-        blended_of = {}
-        blended_of[0] = outs.tile([P, D], F32, name="blended")
+        def bias_out(j):
+            nc.scalar.activation(
+                out=bias_all[:, cols_of(j)], in_=spread_of[j][:], func=ACT.Identity, bias=bg_f32[:, 0:1], scale=1.0
+            )
+
+        transpose_h(0)
+        spread_bias(0)
+        spread_bias(1)
+        transpose_a(0)
+        quantise(0)
+        first_gate_input(0)
+        open_output(0)
         logits(0, 0)
+        spread_bias(2)
+        spread_bias(3)
         gate_value(0, 0)
         role_product(0, 0)
-        transpose_h(1)
-        transpose_a(1)
+        first_gate_input(1)
         logits(0, 1)
-        role_product(0, 1)
+        difference(0, 0)
         gate_value(0, 1)
-        quantise(1)
-        product(0, 0)
-        final_add(0, 0, blended_of[0], nc.gpsimd)
+        role_product(0, 1)
+        first_gate_input(2)
+        difference(0, 1)
+        product_apart(0, 0)
         logits(0, 2)
-        role_product(0, 2)
+        transpose_h(1)
+        first_gate_input(3)
         gate_value(0, 2)
-        product(0, 1)
-        final_add(0, 1, blended_of[0], nc.gpsimd)
-        subtract_on_vector(0, 2)
-        transpose_h(2)
-        transpose_a(2)
+        role_product(0, 2)
+        product_apart(0, 1)
+        quantise(1)
+        final_add(0, slice(0, 2 * SLICE), nc.vector)
+        gate_input(1, slice(0, SLICE))
+        gate_input(1, slice(SLICE, 2 * SLICE))
+        gate_input(1, slice(2 * SLICE, D))
         logits(0, 3)
-        role_product(0, 3)
+        transpose_a(1)
         gate_value(0, 3)
-        subtract_on_vector(0, 3)
-        quantise(2)
-        hold_back(0, 2)
-        hold_back(0, 3)
-
-        def finish_vector_side(i):
-            first = vector_side(i)[0]
-            for j in vector_side(i):
-                from_roles(i, j, blended_of[i])
-            nc.sync.dma_start(out=out_rows[i][:, SLICE * first :], in_=blended_of[i][:, SLICE * first :])
-
-        for i in range(1, ROW_TILES):
+        difference(0, 2)
+        role_product(0, 3)
+        for half in range(2):
+            part_h(2, half)
+        part_a(2)
+        for i in range(0, ROW_TILES):
             last = i == ROW_TILES - 1
-            ahead = i + 2 if i + 2 < ROW_TILES else None
             if not last:
-                start_gate(i + 1)
-            if ahead is not None:
-                transpose_h(ahead)
-                transpose_a(ahead)
-            blended_of[i] = outs.tile([P, D], F32, name="blended")
-            for j in range(S):
-                logits(i, j)
-                role_product(i, j)
-                gate_value(i, j)
-                if j == 0:
-                    finish_vector_side(i - 1)
-                else:
-                    product(i, j - 1)
-                    if last:
-                        final_add(i, j - 1, blended_of[i], nc.gpsimd if j < 3 else nc.vector)
-            subtract_on_vector(i, 3)
-            if ahead is not None:
-                quantise(ahead)
-            hold_back(i, 3)
+                open_output(i + 1)
+                logits(i + 1, 0)
+            if i > 0:
+                role_product(i, 3)
             if not last:
-                tensor_cols = slice(0, 3 * SLICE)
-                nc.vector.tensor_tensor(
-                    out=blended_of[i][:, tensor_cols], in0=gate[i][:, tensor_cols], in1=h_sb[i][:, tensor_cols], op=ADD
-                )
-                nc.sync.dma_start(out=out_rows[i][:, tensor_cols], in_=blended_of[i][:, tensor_cols])
-        finish_vector_side(ROW_TILES - 1)
+                role_product(i + 1, 0)
+                gate_value(i + 1, 0)
+                if 0 in vector_side(i + 1):
+                    difference(i + 1, 0)
+            if i + 2 < ROW_TILES:
+                transpose_h(i + 2)
+                transpose_a(i + 2)
+            difference(i, 3)
+            rest = slice(2 * SLICE if i == 0 else SLICE * len(vector_side(i)), D)
+            if i < ROW_TILES - 2:
+                if 0 in vector_side(i + 1):
+                    hold_back(i + 1, 0)
+                final_add(i, rest, nc.vector)
+                quantise(i + 2)
+                gate_input(i + 2, slice(0, SLICE))
+                gate_input(i + 2, slice(SLICE, D))
+            elif not last:
+                if 0 in vector_side(i + 1):
+                    hold_back(i + 1, 0)
+                for j in range(len(vector_side(i)), S):
+                    final_add(i, cols_of(j), nc.gpsimd)
+            else:
+                final_add(i, slice(2 * SLICE, D), nc.vector)
+            if not last:
+                logits(i + 1, 1)
+                role_product(i + 1, 1)
+                logits(i + 1, 2)
+                logits(i + 1, 3)
+                for j in range(1, S):
+                    if j == 2:
+                        role_product(i + 1, 2)
+                    gate_value(i + 1, j)
+                    if i + 3 < ROW_TILES:
+                        if j < 3:
+                            part_h(i + 3, j - 1)
+                        else:
+                            part_a(i + 3)
+                    if j == 1 and 0 in vector_side(i + 1):
+                        from_roles(i + 1, 0)
+                        store(i + 1, cols_of(0))
+                    else:
+                        difference(i + 1, j - 1)
+                    if i + 1 == ROW_TILES - 1 and j < 3 and j - 1 not in vector_side(i + 1):
+                        final_add(i + 1, cols_of(j - 1), nc.gpsimd)

@@ -21,7 +21,7 @@ SLICE = D // S
 K_PASS = 4 * P
 PASSES = D // K_PASS
 ROW_TILES = B // P
-TR_BANKS, ACC_BANKS, HH_BANKS = 3, 3, 2
+TR_BANKS, ACC_BANKS, HH_BANKS = 2, 3, 2
 
 FLOPS = 2 * B * D * D + 2 * B * ROLES * D
 
@@ -190,7 +190,10 @@ def tile_tpru_pb_kernel(tc, a, vr, h, x2g, w_g_words, w_g_scales, b_g, bg, out):
             return slice(SLICE * j, SLICE * (j + 1))
 
         def role_product(i, j):
-            hh = psum.tile([P, SLICE], F32, tag="hh", bufs=HH_BANKS)
+            if i > 0 and j in vector_side(i):
+                hh = psum.tile([P, SLICE], F32, tag="own", bufs=1)
+            else:
+                hh = psum.tile([P, SLICE], F32, tag="hh", bufs=HH_BANKS)
             hh_of[i, j] = hh
             alone = j in vector_side(i)
             nc.tensor.matmul(hh[:], lhsT=roles_t[i][:, j, :], rhs=vr_sb[:, cols_of(j)], start=True, stop=alone)
@@ -303,12 +306,12 @@ def tile_tpru_pb_kernel(tc, a, vr, h, x2g, w_g_words, w_g_scales, b_g, bg, out):
         difference(0, 0)
         gate_value(0, 1)
         role_product(0, 1)
-        first_gate_input(2)
+        gate_input(0, slice(2 * SLICE, 3 * SLICE))
         difference(0, 1)
         product_apart(0, 0)
         logits(0, 2)
         transpose_h(1)
-        first_gate_input(3)
+        gate_input(0, slice(3 * SLICE, D))
         gate_value(0, 2)
         role_product(0, 2)
         product_apart(0, 1)
@@ -321,59 +324,64 @@ def tile_tpru_pb_kernel(tc, a, vr, h, x2g, w_g_words, w_g_scales, b_g, bg, out):
         transpose_a(1)
         gate_value(0, 3)
         difference(0, 2)
+        if 2 in vector_side(0):
+            product_apart(0, 2)
         role_product(0, 3)
         for half in range(2):
             part_h(2, half)
         part_a(2)
         for i in range(0, ROW_TILES):
             last = i == ROW_TILES - 1
+            own = not last and 0 in vector_side(i + 1)
             if not last:
                 open_output(i + 1)
                 logits(i + 1, 0)
+                role_product(i + 1, 0)
             if i > 0:
                 role_product(i, 3)
             if not last:
-                role_product(i + 1, 0)
                 gate_value(i + 1, 0)
-                if 0 in vector_side(i + 1):
+                if own:
                     difference(i + 1, 0)
             if i + 2 < ROW_TILES:
                 transpose_h(i + 2)
-                transpose_a(i + 2)
+            if last:
+                final_add(i, cols_of(2), nc.vector)
             difference(i, 3)
-            rest = slice(2 * SLICE if i == 0 else SLICE * len(vector_side(i)), D)
             if i < ROW_TILES - 2:
-                if 0 in vector_side(i + 1):
+                if own:
                     hold_back(i + 1, 0)
-                final_add(i, rest, nc.vector)
+                final_add(i, slice(2 * SLICE if i == 0 else SLICE * len(vector_side(i)), D), nc.vector)
                 quantise(i + 2)
                 gate_input(i + 2, slice(0, SLICE))
                 gate_input(i + 2, slice(SLICE, D))
             elif not last:
-                if 0 in vector_side(i + 1):
+                if own:
                     hold_back(i + 1, 0)
                 for j in range(len(vector_side(i)), S):
                     final_add(i, cols_of(j), nc.gpsimd)
             else:
-                final_add(i, slice(2 * SLICE, D), nc.vector)
+                final_add(i, cols_of(3), nc.vector)
             if not last:
                 logits(i + 1, 1)
                 role_product(i + 1, 1)
+                if i + 2 < ROW_TILES:
+                    transpose_a(i + 2)
                 logits(i + 1, 2)
                 logits(i + 1, 3)
                 for j in range(1, S):
-                    if j == 2:
-                        role_product(i + 1, 2)
                     gate_value(i + 1, j)
                     if i + 3 < ROW_TILES:
                         if j < 3:
                             part_h(i + 3, j - 1)
                         else:
                             part_a(i + 3)
-                    if j == 1 and 0 in vector_side(i + 1):
+                    if j == 1 and own:
                         from_roles(i + 1, 0)
                         store(i + 1, cols_of(0))
                     else:
                         difference(i + 1, j - 1)
+                    if j == 1:
+                        role_product(i + 1, 2)
                     if i + 1 == ROW_TILES - 1 and j < 3 and j - 1 not in vector_side(i + 1):
                         final_add(i + 1, cols_of(j - 1), nc.gpsimd)

@@ -166,7 +166,10 @@ def tile_tpru_pb_kernel(tc, a, vr, h, x2g, w_g_words, w_g_scales, b_g, bg, out):
                 )
 
         def transpose_a(i):
-            a_flipped = psum.tile([P, 2, P], F32, tag="tr", bufs=TR_BANKS)
+            if i < 2:
+                a_flipped = psum.tile([P, 2, P], F32, tag="tr", bufs=TR_BANKS)
+            else:
+                a_flipped = psum.tile([P, 2, P], F32, tag="acc", bufs=ACC_BANKS)
             for u in range(2):
                 nc.tensor.transpose(a_flipped[:, u, :], words_of(a_sb, a_apart, i, 0, u), ident[:])
             a_t = prep.tile([P, S, P], BF16, name="a_t")
@@ -284,11 +287,6 @@ def tile_tpru_pb_kernel(tc, a, vr, h, x2g, w_g_words, w_g_scales, b_g, bg, out):
                 op1=ADD,
             )
 
-        def bias_out(j):
-            nc.scalar.activation(
-                out=bias_all[:, cols_of(j)], in_=spread_of[j][:], func=ACT.Identity, bias=bg_f32[:, 0:1], scale=1.0
-            )
-
         transpose_h(0)
         spread_bias(0)
         spread_bias(1)
@@ -345,6 +343,7 @@ def tile_tpru_pb_kernel(tc, a, vr, h, x2g, w_g_words, w_g_scales, b_g, bg, out):
                     difference(i + 1, 0)
             if i + 2 < ROW_TILES:
                 transpose_h(i + 2)
+                transpose_a(i + 2)
             if last:
                 final_add(i, cols_of(2), nc.vector)
             difference(i, 3)
@@ -365,8 +364,6 @@ def tile_tpru_pb_kernel(tc, a, vr, h, x2g, w_g_words, w_g_scales, b_g, bg, out):
             if not last:
                 logits(i + 1, 1)
                 role_product(i + 1, 1)
-                if i + 2 < ROW_TILES:
-                    transpose_a(i + 2)
                 logits(i + 1, 2)
                 logits(i + 1, 3)
                 for j in range(1, S):

@@ -43,7 +43,7 @@ def tile_tpru_pb_kernel(tc, a, vr, h, x2g, w_g_words, w_g_scales, b_g, bg, out):
         rows = ctx.enter_context(tc.tile_pool(name="rows", bufs=ROW_TILES))
         prep = ctx.enter_context(tc.tile_pool(name="prep", bufs=3))
         gates = ctx.enter_context(tc.tile_pool(name="gates", bufs=2))
-        outs = ctx.enter_context(tc.tile_pool(name="outs", bufs=3))
+        outs = ctx.enter_context(tc.tile_pool(name="outs", bufs=6))
         work = ctx.enter_context(tc.tile_pool(name="work", bufs=3))
         psum = ctx.enter_context(tc.psum_pool(name="psum", bufs=2))
         ctx.enter_context(tc.manual_schedule())
@@ -328,7 +328,7 @@ def tile_tpru_pb_kernel(tc, a, vr, h, x2g, w_g_words, w_g_scales, b_g, bg, out):
         for half in range(2):
             part_h(2, half)
         part_a(2)
-        for i in range(0, ROW_TILES):
+        for i in range(0, ROW_TILES - 2):
             last = i == ROW_TILES - 1
             own = not last and 0 in vector_side(i + 1)
             if not last:
@@ -339,8 +339,10 @@ def tile_tpru_pb_kernel(tc, a, vr, h, x2g, w_g_words, w_g_scales, b_g, bg, out):
                 role_product(i, 3)
             if not last:
                 gate_value(i + 1, 0)
-                if own:
-                    difference(i + 1, 0)
+            if i > 0:
+                difference(i, 2)
+            if own:
+                difference(i + 1, 0)
             if i + 2 < ROW_TILES:
                 transpose_h(i + 2)
                 transpose_a(i + 2)
@@ -365,20 +367,50 @@ def tile_tpru_pb_kernel(tc, a, vr, h, x2g, w_g_words, w_g_scales, b_g, bg, out):
                 logits(i + 1, 1)
                 role_product(i + 1, 1)
                 logits(i + 1, 2)
+                role_product(i + 1, 2)
                 logits(i + 1, 3)
-                for j in range(1, S):
-                    gate_value(i + 1, j)
-                    if i + 3 < ROW_TILES:
-                        if j < 3:
-                            part_h(i + 3, j - 1)
-                        else:
-                            part_a(i + 3)
-                    if j == 1 and own:
-                        from_roles(i + 1, 0)
-                        store(i + 1, cols_of(0))
-                    else:
-                        difference(i + 1, j - 1)
-                    if j == 1:
-                        role_product(i + 1, 2)
-                    if i + 1 == ROW_TILES - 1 and j < 3 and j - 1 not in vector_side(i + 1):
-                        final_add(i + 1, cols_of(j - 1), nc.gpsimd)
+                gate_value(i + 1, 1)
+                if i + 3 < ROW_TILES:
+                    part_h(i + 3, 0)
+                if own:
+                    from_roles(i + 1, 0)
+                    store(i + 1, cols_of(0))
+                else:
+                    difference(i + 1, 0)
+                gate_value(i + 1, 2)
+                gate_value(i + 1, 3)
+                if i + 3 < ROW_TILES:
+                    part_h(i + 3, 1)
+                difference(i + 1, 1)
+                if i + 3 < ROW_TILES:
+                    part_a(i + 3)
+                if i + 1 == ROW_TILES - 1:
+                    final_add(i + 1, cols_of(1), nc.gpsimd)
+        open_output(7)
+        logits(7, 0)
+        role_product(7, 0)
+        role_product(6, 3)
+        gate_value(7, 0)
+        difference(6, 2)
+        difference(7, 0)
+        difference(6, 3)
+        hold_back(7, 0)
+        final_add(6, slice(SLICE * 3, SLICE * 4), nc.gpsimd)
+        final_add(6, slice(SLICE * 1, SLICE * 2), nc.gpsimd)
+        final_add(6, slice(SLICE * 2, SLICE * 3), nc.gpsimd)
+        logits(7, 1)
+        role_product(7, 1)
+        logits(7, 2)
+        role_product(7, 2)
+        logits(7, 3)
+        gate_value(7, 1)
+        from_roles(7, 0)
+        store(7, cols_of(0))
+        gate_value(7, 2)
+        difference(7, 1)
+        gate_value(7, 3)
+        role_product(7, 3)
+        difference(7, 2)
+        final_add(7, slice(SLICE * 1, SLICE * 3), nc.vector)
+        difference(7, 3)
+        final_add(7, slice(SLICE * 3, SLICE * 4), nc.vector)

@@ -53,8 +53,10 @@ def tile_tpru_pb_kernel(tc, a, vr, h, x2g, w_g_words, w_g_scales, b_g, bg, out):
         nc.scalar.activation(out=warm[:, 1:2], in_=warm[:, 0:1], func=ACT.Sigmoid)
         bias_row = const.tile([P, D], BF16)
         nc.vector.memset(bias_row[:].bitcast(I32), 0)
-        w_planes = const.tile([P, PASSES, D], U8, align_bytes=64)
-        nc.vector.memset(w_planes[:].rearrange("p g n -> p (g n)").bitcast(I32), 0)
+        w_planes = {}
+        for half in range(2):
+            w_planes[half] = const.tile([P, PASSES, D // 2], U8, align_bytes=64, name="w_planes_%d" % half)
+            nc.vector.memset(w_planes[half][:].rearrange("p g n -> p (g n)").bitcast(I32), 0)
         ident = const.tile([P, P], F32)
         make_identity(nc, ident[:])
         ones = const.tile([P, P], BF16)
@@ -64,9 +66,10 @@ def tile_tpru_pb_kernel(tc, a, vr, h, x2g, w_g_words, w_g_scales, b_g, bg, out):
 
         h_sb, x2g_sb, a_sb = {}, {}, {}
 
-        def load_h(i):
-            h_sb[i] = rows.tile([P, D], BF16, name="h_tile")
-            nc.sync.dma_start(out=h_sb[i][:], in_=h_rows[i])
+        def load_h(i, cols=slice(0, D)):
+            if i not in h_sb:
+                h_sb[i] = rows.tile([P, D], BF16, name="h_tile")
+            nc.sync.dma_start(out=h_sb[i][:, cols], in_=h_rows[i][:, cols])
 
         def load_a(i):
             a_sb[i] = rows.tile([P, ROLES * S], BF16, name="a_tile")
@@ -92,27 +95,34 @@ def tile_tpru_pb_kernel(tc, a, vr, h, x2g, w_g_words, w_g_scales, b_g, bg, out):
                 in_=words_by_partition[:, :, 2 * SLICE * j : 2 * SLICE * (j + 1)].bitcast(I32),
             )
 
+        scales_by_row = w_g_scales.rearrange("g q n -> q g n")
+
+        def load_scales(half):
+            cols = slice(D // 2 * half, D // 2 * (half + 1))
+            for r in range(4):
+                nc.sync.dma_start(
+                    out=w_planes[half][r:P:32, :, :].bitcast(I32), in_=scales_by_row[r:16:4, :, cols].bitcast(I32)
+                )
+
         load_h(0)
         load_a(0)
-        load_w(0)
         nc.sync.dma_start(out=bias_row[0:1, :], in_=b_g.unsqueeze(0))
         bg_bf16 = const.tile([P, 1], BF16)
         nc.sync.dma_start(out=bg_bf16[:], in_=bg.partition_broadcast(P))
-        scales_by_row = w_g_scales.rearrange("g q n -> q g n")
-        for r in range(4):
-            nc.sync.dma_start(
-                out=w_planes[r:P:32, :, :].bitcast(I32),
-                in_=scales_by_row[r:16:4].bitcast(I32),
-            )
-        for j in range(S):
-            if j > 0:
-                load_w(j)
-            if j == 2:
-                load_h(1)
-            load_x2g(0, slice(SLICE * j, SLICE * (j + 1)))
-            load_vr(slice(SLICE * j, SLICE * (j + 1)))
+        load_w(0)
+        load_scales(0)
+        load_x2g(0, slice(SLICE * 0, SLICE * 2))
+        load_vr(slice(SLICE * 0, SLICE * 2))
+        load_w(1)
+        load_h(1)
         load_a(1)
-        load_x2g(1)
+        load_x2g(0, slice(SLICE * 2, SLICE * 4))
+        load_scales(1)
+        load_w(2)
+        load_vr(slice(SLICE * 2, SLICE * 4))
+        load_x2g(1, slice(SLICE * 0, SLICE * 2))
+        load_w(3)
+        load_x2g(1, slice(SLICE * 2, SLICE * 4))
         for i in range(2, ROW_TILES):
             load_h(i)
             load_a(i)
@@ -182,10 +192,17 @@ def tile_tpru_pb_kernel(tc, a, vr, h, x2g, w_g_words, w_g_scales, b_g, bg, out):
             )
             roles_t[i] = a_t
 
-        def quantise(i):
+        def quantise(i, parts=1):
             codes = prep.tile([P, PASSES * P], U32, align_bytes=64, name="codes")
             planes = prep.tile([P, PASSES * P], U8, align_bytes=64, name="planes")
-            nc.vector.quantize_mx(out=codes[:].bitcast(FP8X4), scales=planes[:], in_=grouped_of[i][:])
+            width = PASSES * P // parts
+            for part in range(parts):
+                cols = slice(width * part, width * (part + 1))
+                nc.vector.quantize_mx(
+                    out=codes[:, cols].bitcast(FP8X4),
+                    scales=planes[:, cols],
+                    in_=grouped_of[i][:, 4 * width * part : 4 * width * (part + 1)],
+                )
             h_codes[i] = codes
             h_planes[i] = planes
 
@@ -213,7 +230,7 @@ def tile_tpru_pb_kernel(tc, a, vr, h, x2g, w_g_words, w_g_scales, b_g, bg, out):
                     lhsT=h_codes[i][:, rows_g].bitcast(FP8X4),
                     lhsT_scale=h_planes[i][:, rows_g],
                     rhs=w_words[j][:, g, :].bitcast(FP4X4),
-                    rhs_scale=w_planes[:, g, cols_of(j)],
+                    rhs_scale=w_planes[j // 2][:, g, SLICE * (j % 2) : SLICE * (j % 2 + 1)],
                     start=(g == 0),
                     stop=(g == PASSES - 1),
                 )
@@ -304,29 +321,27 @@ def tile_tpru_pb_kernel(tc, a, vr, h, x2g, w_g_words, w_g_scales, b_g, bg, out):
         difference(0, 0)
         gate_value(0, 1)
         role_product(0, 1)
-        gate_input(0, slice(2 * SLICE, 3 * SLICE))
+        gate_input(0, slice(SLICE * 2, SLICE * 3))
         difference(0, 1)
         product_apart(0, 0)
-        logits(0, 2)
         transpose_h(1)
-        gate_input(0, slice(3 * SLICE, D))
-        gate_value(0, 2)
-        role_product(0, 2)
+        transpose_a(1)
+        gate_input(0, slice(SLICE * 3, SLICE * 4))
         product_apart(0, 1)
         quantise(1)
-        final_add(0, slice(0, 2 * SLICE), nc.vector)
-        gate_input(1, slice(0, SLICE))
-        gate_input(1, slice(SLICE, 2 * SLICE))
-        gate_input(1, slice(2 * SLICE, D))
+        final_add(0, slice(SLICE * 0, SLICE * 2), nc.vector)
+        logits(0, 2)
+        gate_value(0, 2)
+        role_product(0, 2)
+        gate_input(1, slice(SLICE * 0, SLICE * 1))
+        gate_input(1, slice(SLICE * 1, SLICE * 2))
+        gate_input(1, slice(SLICE * 2, SLICE * 4))
         logits(0, 3)
-        transpose_a(1)
         gate_value(0, 3)
         difference(0, 2)
-        if 2 in vector_side(0):
-            product_apart(0, 2)
         role_product(0, 3)
-        for half in range(2):
-            part_h(2, half)
+        part_h(2, 0)
+        part_h(2, 1)
         part_a(2)
         for i in range(0, ROW_TILES - 2):
             last = i == ROW_TILES - 1

@@ -269,10 +269,10 @@ def tile_tpru_pb_kernel(tc, a, vr, h, x2g, w_g_words, w_g_scales, b_g, bg, out):
             engine.tensor_tensor(out=blended_of[i][:, cols], in0=gate[i][:, cols], in1=h_sb[i][:, cols], op=ADD)
             store(i, cols)
 
-        def gate_input(i, cols):
+        def gate_input(i, cols, engine=nc.gpsimd):
             if i not in gate:
                 gate[i] = gates.tile([P, D], F32, name="gate")
-            nc.gpsimd.tensor_tensor(out=gate[i][:, cols], in0=x2g_sb[i][:, cols], in1=bias_all[:, cols], op=ADD)
+            engine.tensor_tensor(out=gate[i][:, cols], in0=x2g_sb[i][:, cols], in1=bias_all[:, cols], op=ADD)
 
         blended_of = {}
 
@@ -336,12 +336,12 @@ def tile_tpru_pb_kernel(tc, a, vr, h, x2g, w_g_words, w_g_scales, b_g, bg, out):
         gate_input(1, slice(SLICE * 0, SLICE * 1))
         gate_input(1, slice(SLICE * 1, SLICE * 2))
         gate_input(1, slice(SLICE * 2, SLICE * 4))
+        part_h(2, 0)
+        part_h(2, 1)
         logits(0, 3)
         gate_value(0, 3)
         difference(0, 2)
         role_product(0, 3)
-        part_h(2, 0)
-        part_h(2, 1)
         part_a(2)
         for i in range(0, ROW_TILES - 2):
             last = i == ROW_TILES - 1
@@ -426,6 +426,7 @@ def tile_tpru_pb_kernel(tc, a, vr, h, x2g, w_g_words, w_g_scales, b_g, bg, out):
         gate_value(7, 3)
         role_product(7, 3)
         difference(7, 2)
-        final_add(7, slice(SLICE * 1, SLICE * 3), nc.vector)
+        final_add(7, slice(SLICE * 1, SLICE * 2), nc.vector)
         difference(7, 3)
+        final_add(7, slice(SLICE * 2, SLICE * 3), nc.vector)
         final_add(7, slice(SLICE * 3, SLICE * 4), nc.vector)

@@ -114,9 +114,9 @@ def tile_tpru_pb_kernel(tc, a, vr, h, x2g, w_g_words, w_g_scales, b_g, bg, out):
         load_x2g(0, slice(SLICE * 0, SLICE * 2))
         load_vr(slice(SLICE * 0, SLICE * 2))
         load_w(1)
+        load_x2g(0, slice(SLICE * 2, SLICE * 4))
         load_h(1)
         load_a(1)
-        load_x2g(0, slice(SLICE * 2, SLICE * 4))
         load_scales(1)
         load_w(2)
         load_vr(slice(SLICE * 2, SLICE * 4))
@@ -339,10 +339,10 @@ def tile_tpru_pb_kernel(tc, a, vr, h, x2g, w_g_words, w_g_scales, b_g, bg, out):
         part_h(2, 0)
         part_h(2, 1)
         logits(0, 3)
-        gate_value(0, 3)
         difference(0, 2)
         role_product(0, 3)
         part_a(2)
+        gate_value(0, 3)
         for i in range(0, ROW_TILES - 2):
             last = i == ROW_TILES - 1
             own = not last and 0 in vector_side(i + 1)

@@ -130,10 +130,12 @@ def tile_tpru_pb_kernel(tc, a, vr, h, x2g, w_g_words, w_g_scales, b_g, bg, out):
 
         minus_ident = const.tile([P, P], BF16)
         nc.vector.tensor_scalar_mul(out=minus_ident[:], in0=ident_bf16[:], scalar1=-1.0)
-        bg_f32 = const.tile([P, 1], F32)
-        nc.vector.tensor_copy(out=bg_f32[:], in_=bg_bf16[:])
+        bg_of = {}
+        for sign in (1.0, -1.0):
+            bg_of[sign] = const.tile([P, 1], F32, name="bg_plus" if sign > 0 else "bg_minus")
+            nc.vector.tensor_scalar_mul(out=bg_of[sign][:], in0=bg_bf16[:], scalar1=sign)
 
-        bias_all = const.tile([P, D], F32)
+        bias_all = const.tile([P, D], BF16)
 
         h_codes, h_planes, roles_t, grouped_of, gate, hh_of, acc_of, diff_sb = {}, {}, {}, {}, {}, {}, {}, {}
 
@@ -238,7 +240,8 @@ def tile_tpru_pb_kernel(tc, a, vr, h, x2g, w_g_words, w_g_scales, b_g, bg, out):
         def gate_value(i, j):
             g_cols = gate[i][:, cols_of(j)]
             nc.vector.tensor_tensor(out=g_cols, in0=acc_of[i, j][:], in1=g_cols, op=ADD)
-            nc.scalar.activation(out=g_cols, in_=g_cols, func=ACT.Sigmoid, scale=-1.0 if i > 0 and j in vector_side(i) else 1.0)
+            sign = -1.0 if i > 0 and j in vector_side(i) else 1.0
+            nc.scalar.activation(out=g_cols, in_=g_cols, func=ACT.Sigmoid, bias=bg_of[sign][:, 0:1], scale=sign)
 
         def difference(i, j):
             if j in vector_side(i):
@@ -288,20 +291,13 @@ def tile_tpru_pb_kernel(tc, a, vr, h, x2g, w_g_words, w_g_scales, b_g, bg, out):
                 spread = psum.tile([P, SLICE], F32, tag="tr", bufs=TR_BANKS)
             spread_of[j] = spread
             nc.tensor.matmul(spread[:], lhsT=ones[:], rhs=bias_row[:, cols_of(j)], start=True, stop=True)
-            nc.scalar.activation(
-                out=bias_all[:, cols_of(j)], in_=spread[:], func=ACT.Identity, bias=bg_f32[:, 0:1], scale=1.0
-            )
+            nc.scalar.copy(out=bias_all[:, cols_of(j)], in_=spread[:])
 
         gate[0] = gates.tile([P, D], F32, name="gate")
 
         def first_gate_input(j):
-            nc.vector.scalar_tensor_tensor(
-                out=gate[0][:, cols_of(j)],
-                in0=spread_of[j][:],
-                scalar=bg_f32[:, 0:1],
-                in1=x2g_sb[0][:, cols_of(j)],
-                op0=ADD,
-                op1=ADD,
+            nc.vector.tensor_tensor(
+                out=gate[0][:, cols_of(j)], in0=spread_of[j][:], in1=x2g_sb[0][:, cols_of(j)], op=ADD
             )
 
         transpose_h(0)

@@ -120,8 +120,8 @@ def tile_tpru_pb_kernel(tc, a, vr, h, x2g, w_g_words, w_g_scales, b_g, bg, out):
         load_scales(1)
         load_w(2)
         load_vr(slice(SLICE * 2, SLICE * 4))
-        load_x2g(1, slice(SLICE * 0, SLICE * 2))
         load_w(3)
+        load_x2g(1, slice(SLICE * 0, SLICE * 2))
         load_x2g(1, slice(SLICE * 2, SLICE * 4))
         for i in range(2, ROW_TILES):
             load_h(i)
@@ -317,20 +317,18 @@ def tile_tpru_pb_kernel(tc, a, vr, h, x2g, w_g_words, w_g_scales, b_g, bg, out):
         difference(0, 0)
         gate_value(0, 1)
         role_product(0, 1)
-        gate_input(0, slice(SLICE * 2, SLICE * 3))
+        gate_input(0, slice(SLICE * 2, SLICE * 4))
         difference(0, 1)
         product_apart(0, 0)
         transpose_h(1)
         transpose_a(1)
-        gate_input(0, slice(SLICE * 3, SLICE * 4))
         product_apart(0, 1)
         quantise(1)
         final_add(0, slice(SLICE * 0, SLICE * 2), nc.vector)
         logits(0, 2)
         gate_value(0, 2)
         role_product(0, 2)
-        gate_input(1, slice(SLICE * 0, SLICE * 1))
-        gate_input(1, slice(SLICE * 1, SLICE * 2))
+        gate_input(1, slice(SLICE * 0, SLICE * 2))
         gate_input(1, slice(SLICE * 2, SLICE * 4))
         part_h(2, 0)
         part_h(2, 1)
@@ -412,8 +410,8 @@ def tile_tpru_pb_kernel(tc, a, vr, h, x2g, w_g_words, w_g_scales, b_g, bg, out):
         logits(7, 1)
         role_product(7, 1)
         logits(7, 2)
-        role_product(7, 2)
         logits(7, 3)
+        role_product(7, 2)
         gate_value(7, 1)
         from_roles(7, 0)
         store(7, cols_of(0))

from contextlib import ExitStack

import concourse.mybir as mybir
from concourse.masks import make_identity

F32 = mybir.dt.float32
BF16 = mybir.dt.bfloat16
I32 = mybir.dt.int32
U32 = mybir.dt.uint32
U8 = mybir.dt.uint8
FP8X4 = mybir.dt.float8_e4m3fn_x4
FP4X4 = mybir.dt.float4_e2m1fn_x4
ADD = mybir.AluOpType.add
SUBTRACT = mybir.AluOpType.subtract
MULT = mybir.AluOpType.mult
ACT = mybir.ActivationFunctionType

P = 128
B, D, S, ROLES = 1024, 2048, 4, 128
SLICE = D // S
K_PASS = 4 * P
PASSES = D // K_PASS
ROW_TILES = B // P
TR_BANKS, ACC_BANKS, HH_BANKS = 2, 3, 2

FLOPS = 2 * B * D * D + 2 * B * ROLES * D


def vector_side(i):
    return (0, 1) if i == 0 else (0,)


def tile_tpru_pb_kernel(tc, a, vr, h, x2g, w_g_words, w_g_scales, b_g, bg, out):
    nc = tc.nc
    h_rows = h.rearrange("(i p) d -> i p d", p=P)
    x2g_rows = x2g.rearrange("(i p) d -> i p d", p=P)
    a_rows = a.rearrange("(i p) n s -> i p (n s)", p=P)
    out_rows = out.rearrange("(i p) d -> i p d", p=P)
    vr_rows = vr.rearrange("n s d -> n (s d)")

    with ExitStack() as ctx:
        const = ctx.enter_context(tc.tile_pool(name="const", bufs=1))
        rows = ctx.enter_context(tc.tile_pool(name="rows", bufs=ROW_TILES))
        prep = ctx.enter_context(tc.tile_pool(name="prep", bufs=3))
        gates = ctx.enter_context(tc.tile_pool(name="gates", bufs=2))
        outs = ctx.enter_context(tc.tile_pool(name="outs", bufs=6))
        work = ctx.enter_context(tc.tile_pool(name="work", bufs=3))
        psum = ctx.enter_context(tc.psum_pool(name="psum", bufs=2))
        ctx.enter_context(tc.manual_schedule())

        warm = const.tile([P, 2], F32)
        nc.vector.memset(warm[:], 0.0)
        nc.scalar.activation(out=warm[:, 1:2], in_=warm[:, 0:1], func=ACT.Sigmoid)
        bias_row = const.tile([P, D], BF16)
        nc.vector.memset(bias_row[:].bitcast(I32), 0)
        w_planes = {}
        for half in range(2):
            w_planes[half] = const.tile([P, PASSES, D // 2], U8, align_bytes=64, name="w_planes_%d" % half)
            nc.vector.memset(w_planes[half][:].rearrange("p g n -> p (g n)").bitcast(I32), 0)
        ident = const.tile([P, P], F32)
        make_identity(nc, ident[:])
        ones = const.tile([P, P], BF16)
        nc.gpsimd.memset(ones[:], 1.0)
        ident_bf16 = const.tile([P, P], BF16)
        make_identity(nc, ident_bf16[:])

        h_sb, x2g_sb, a_sb = {}, {}, {}

        def load_h(i, cols=slice(0, D)):
            if i not in h_sb:
                h_sb[i] = rows.tile([P, D], BF16, name="h_tile")
            nc.sync.dma_start(out=h_sb[i][:, cols], in_=h_rows[i][:, cols])

        def load_a(i):
            a_sb[i] = rows.tile([P, ROLES * S], BF16, name="a_tile")
            nc.sync.dma_start(out=a_sb[i][:], in_=a_rows[i])

        def load_x2g(i, cols=slice(0, D)):
            if i not in x2g_sb:
                x2g_sb[i] = rows.tile([P, D], BF16, name="x2g_tile")
            nc.sync.dma_start(out=x2g_sb[i][:, cols], in_=x2g_rows[i][:, cols])

        vr_sb = const.tile([P, D], BF16)

        def load_vr(cols):
            nc.sync.dma_start(out=vr_sb[:, cols], in_=vr_rows[:, cols])

        w_words = {}
        words_by_partition = w_g_words.rearrange("g p c -> p g c")

        def load_w(j):
            w_words[j] = const.tile([P, PASSES, 2 * SLICE], U8, align_bytes=64, name="w_words_%d" % j)
            nc.sync.dma_start(
                out=w_words[j][:].bitcast(I32),
                in_=words_by_partition[:, :, 2 * SLICE * j : 2 * SLICE * (j + 1)].bitcast(I32),
            )

        scales_by_row = w_g_scales.rearrange("g q n -> q g n")

        def load_scales(half):
            cols = slice(D // 2 * half, D // 2 * (half + 1))
            for r in range(4):
                nc.sync.dma_start(
                    out=w_planes[half][r:P:32, :, :].bitcast(I32), in_=scales_by_row[r:16:4, :, cols].bitcast(I32)
                )

        load_h(0)
        load_a(0)
        nc.sync.dma_start(out=bias_row[0:1, :], in_=b_g.unsqueeze(0))
        bg_bf16 = const.tile([P, 1], BF16)
        nc.sync.dma_start(out=bg_bf16[:], in_=bg.partition_broadcast(P))
        load_w(0)
        load_scales(0)
        load_x2g(0, slice(SLICE * 0, SLICE * 2))
        load_vr(slice(SLICE * 0, SLICE * 2))
        load_w(1)
        load_x2g(0, slice(SLICE * 2, SLICE * 4))
        load_h(1)
        load_a(1)
        load_scales(1)
        load_w(2)
        load_vr(slice(SLICE * 2, SLICE * 4))
        load_w(3)
        load_x2g(1, slice(SLICE * 0, SLICE * 2))
        load_x2g(1, slice(SLICE * 2, SLICE * 4))
        for i in range(2, ROW_TILES):
            load_h(i)
            load_a(i)
            load_x2g(i)

        minus_ident = const.tile([P, P], BF16)
        nc.vector.tensor_scalar_mul(out=minus_ident[:], in0=ident_bf16[:], scalar1=-1.0)
        bg_of = {}
        for sign in (1.0, -1.0):
            bg_of[sign] = const.tile([P, 1], F32, name="bg_plus" if sign > 0 else "bg_minus")
            nc.vector.tensor_scalar_mul(out=bg_of[sign][:], in0=bg_bf16[:], scalar1=sign)

        bias_all = const.tile([P, D], BF16)

        h_codes, h_planes, roles_t, grouped_of, gate, hh_of, acc_of, diff_sb = {}, {}, {}, {}, {}, {}, {}, {}

        h_apart, a_apart = {}, {}

        def part_h(i, half):
            if i not in h_apart:
                h_apart[i] = prep.tile([P, D], BF16, name="h_apart")
            words = slice(D // 4 * half, D // 4 * (half + 1))
            nc.scalar.copy(
                out=h_apart[i][:].bitcast(F32)[:, words].rearrange("p (g u w) -> p g u w", u=2, w=P),
                in_=h_sb[i][:].bitcast(F32)[:, words].rearrange("p (g w u) -> p g u w", u=2, w=P),
            )

        def part_a(i):
            a_apart[i] = prep.tile([P, ROLES * S], BF16, name="a_apart")
            nc.scalar.copy(
                out=a_apart[i][:].bitcast(F32).rearrange("p (u n) -> p u n", u=2),
                in_=a_sb[i][:].bitcast(F32).rearrange("p (n u) -> p u n", u=2),
            )

        def words_of(source, apart, i, start, u):
            if i in apart:
                return apart[i][:].bitcast(F32)[:, start + P * u : start + P * (u + 1)]
            return source[i][:].bitcast(F32)[:, start + u : start + 2 * P : 2]

        def transpose_h(i):
            grouped = prep.tile([P, D], BF16, align_bytes=64, name="grouped")
            grouped_of[i] = grouped
            grouped_words = grouped[:].bitcast(F32).rearrange("p (g b u) -> p g b u", g=PASSES, b=P, u=2)
            for half in range(2):
                flipped = psum.tile([P, 2, 2, P], F32, tag="tr", bufs=TR_BANKS)
                for gg in range(2):
                    g = 2 * half + gg
                    for u in range(2):
                        nc.tensor.transpose(flipped[:, gg, u, :], words_of(h_sb, h_apart, i, 2 * P * g, u), ident[:])
                nc.scalar.copy(
                    out=grouped_words[:, 2 * half : 2 * half + 2, :, :],
                    in_=flipped[:].rearrange("p g u b -> p g b u"),
                )

        def transpose_a(i):
            if i < 2:
                a_flipped = psum.tile([P, 2, P], F32, tag="tr", bufs=TR_BANKS)
            else:
                a_flipped = psum.tile([P, 2, P], F32, tag="acc", bufs=ACC_BANKS)
            for u in range(2):
                nc.tensor.transpose(a_flipped[:, u, :], words_of(a_sb, a_apart, i, 0, u), ident[:])
            a_t = prep.tile([P, S, P], BF16, name="a_t")
            nc.scalar.copy(
                out=a_t[:].rearrange("n (u e) b -> n u e b", u=2),
                in_=a_flipped[:]
                .rearrange("n u b -> n (u b)")
                .bitcast(BF16)
                .rearrange("n (u b e) -> n u e b", u=2, b=P, e=2),
            )
            roles_t[i] = a_t

        def quantise(i, parts=1):
            codes = prep.tile([P, PASSES * P], U32, align_bytes=64, name="codes")
            planes = prep.tile([P, PASSES * P], U8, align_bytes=64, name="planes")
            width = PASSES * P // parts
            for part in range(parts):
                cols = slice(width * part, width * (part + 1))
                nc.vector.quantize_mx(
                    out=codes[:, cols].bitcast(FP8X4),
                    scales=planes[:, cols],
                    in_=grouped_of[i][:, 4 * width * part : 4 * width * (part + 1)],
                )
            h_codes[i] = codes
            h_planes[i] = planes

        def cols_of(j):
            return slice(SLICE * j, SLICE * (j + 1))

        def role_product(i, j):
            if i > 0 and j in vector_side(i):
                hh = psum.tile([P, SLICE], F32, tag="own", bufs=1)
            else:
                hh = psum.tile([P, SLICE], F32, tag="hh", bufs=HH_BANKS)
            hh_of[i, j] = hh
            alone = j in vector_side(i)
            nc.tensor.matmul(hh[:], lhsT=roles_t[i][:, j, :], rhs=vr_sb[:, cols_of(j)], start=True, stop=alone)
            if not alone:
                nc.tensor.matmul(hh[:], lhsT=minus_ident[:], rhs=h_sb[i][:, cols_of(j)], start=False, stop=True)

        def logits(i, j):
            acc = psum.tile([P, SLICE], F32, tag="acc", bufs=ACC_BANKS)
            acc_of[i, j] = acc
            for g in range(PASSES):
                rows_g = slice(P * g, P * (g + 1))
                nc.tensor.matmul_mx(
                    out=acc[:],
                    lhsT=h_codes[i][:, rows_g].bitcast(FP8X4),
                    lhsT_scale=h_planes[i][:, rows_g],
                    rhs=w_words[j][:, g, :].bitcast(FP4X4),
                    rhs_scale=w_planes[j // 2][:, g, SLICE * (j % 2) : SLICE * (j % 2 + 1)],
                    start=(g == 0),
                    stop=(g == PASSES - 1),
                )

        def gate_value(i, j):
            g_cols = gate[i][:, cols_of(j)]
            nc.vector.tensor_tensor(out=g_cols, in0=acc_of[i, j][:], in1=g_cols, op=ADD)
            sign = -1.0 if i > 0 and j in vector_side(i) else 1.0
            nc.scalar.activation(out=g_cols, in_=g_cols, func=ACT.Sigmoid, bias=bg_of[sign][:, 0:1], scale=sign)

        def difference(i, j):
            if j in vector_side(i):
                diff = work.tile([P, SLICE], F32, name="diff")
                diff_sb[i, j] = diff
                nc.vector.tensor_tensor(out=diff[:], in0=hh_of[i, j][:], in1=h_sb[i][:, cols_of(j)], op=SUBTRACT)
            else:
                g_cols = gate[i][:, cols_of(j)]
                nc.vector.tensor_tensor(out=g_cols, in0=hh_of[i, j][:], in1=g_cols, op=MULT)

        def hold_back(i, j):
            diff = diff_sb[i, j]
            nc.vector.tensor_tensor(out=diff[:], in0=diff[:], in1=gate[i][:, cols_of(j)], op=MULT)

        def product_apart(i, j):
            g_cols = gate[i][:, cols_of(j)]
            nc.vector.tensor_tensor(out=g_cols, in0=diff_sb[i, j][:], in1=g_cols, op=MULT)

        def from_roles(i, j):
            nc.vector.tensor_tensor(
                out=blended_of[i][:, cols_of(j)], in0=hh_of[i, j][:], in1=diff_sb[i, j][:], op=SUBTRACT
            )

        def store(i, cols):
            nc.sync.dma_start(out=out_rows[i][:, cols], in_=blended_of[i][:, cols])

        def final_add(i, cols, engine):
            engine.tensor_tensor(out=blended_of[i][:, cols], in0=gate[i][:, cols], in1=h_sb[i][:, cols], op=ADD)
            store(i, cols)

        def gate_input(i, cols, engine=nc.gpsimd):
            if i not in gate:
                gate[i] = gates.tile([P, D], F32, name="gate")
            engine.tensor_tensor(out=gate[i][:, cols], in0=x2g_sb[i][:, cols], in1=bias_all[:, cols], op=ADD)

        blended_of = {}

        def open_output(i):
            blended_of[i] = outs.tile([P, D], F32, name="blended")

        spread_of = {}

        def spread_bias(j):
            if j < 2:
                spread = psum.tile([P, SLICE], F32, tag="hh", bufs=HH_BANKS)
            else:
                spread = psum.tile([P, SLICE], F32, tag="tr", bufs=TR_BANKS)
            spread_of[j] = spread
            nc.tensor.matmul(spread[:], lhsT=ones[:], rhs=bias_row[:, cols_of(j)], start=True, stop=True)
            nc.scalar.copy(out=bias_all[:, cols_of(j)], in_=spread[:])

        gate[0] = gates.tile([P, D], F32, name="gate")

        def first_gate_input(j):
            nc.vector.tensor_tensor(
                out=gate[0][:, cols_of(j)], in0=spread_of[j][:], in1=x2g_sb[0][:, cols_of(j)], op=ADD
            )

        transpose_h(0)
        spread_bias(0)
        spread_bias(1)
        transpose_a(0)
        quantise(0)
        first_gate_input(0)
        open_output(0)
        logits(0, 0)
        spread_bias(2)
        spread_bias(3)
        gate_value(0, 0)
        role_product(0, 0)
        first_gate_input(1)
        logits(0, 1)
        difference(0, 0)
        gate_value(0, 1)
        role_product(0, 1)
        gate_input(0, slice(SLICE * 2, SLICE * 4))
        difference(0, 1)
        product_apart(0, 0)
        transpose_h(1)
        transpose_a(1)
        product_apart(0, 1)
        quantise(1)
        final_add(0, slice(SLICE * 0, SLICE * 2), nc.vector)
        logits(0, 2)
        gate_value(0, 2)
        role_product(0, 2)
        gate_input(1, slice(SLICE * 0, SLICE * 2))
        gate_input(1, slice(SLICE * 2, SLICE * 4))
        part_h(2, 0)
        part_h(2, 1)
        logits(0, 3)
        difference(0, 2)
        role_product(0, 3)
        part_a(2)
        gate_value(0, 3)
        for i in range(0, ROW_TILES - 2):
            last = i == ROW_TILES - 1
            own = not last and 0 in vector_side(i + 1)
            if not last:
                open_output(i + 1)
                logits(i + 1, 0)
                role_product(i + 1, 0)
            if i > 0:
                role_product(i, 3)
            if not last:
                gate_value(i + 1, 0)
            if i > 0:
                difference(i, 2)
            if own:
                difference(i + 1, 0)
            if i + 2 < ROW_TILES:
                transpose_h(i + 2)
                transpose_a(i + 2)
            if last:
                final_add(i, cols_of(2), nc.vector)
            difference(i, 3)
            if i < ROW_TILES - 2:
                if own:
                    hold_back(i + 1, 0)
                final_add(i, slice(2 * SLICE if i == 0 else SLICE * len(vector_side(i)), D), nc.vector)
                quantise(i + 2)
                gate_input(i + 2, slice(0, SLICE))
                gate_input(i + 2, slice(SLICE, D))
            elif not last:
                if own:
                    hold_back(i + 1, 0)
                for j in range(len(vector_side(i)), S):
                    final_add(i, cols_of(j), nc.gpsimd)
            else:
                final_add(i, cols_of(3), nc.vector)
            if not last:
                logits(i + 1, 1)
                role_product(i + 1, 1)
                logits(i + 1, 2)
                role_product(i + 1, 2)
                logits(i + 1, 3)
                gate_value(i + 1, 1)
                if i + 3 < ROW_TILES:
                    part_h(i + 3, 0)
                if own:
                    from_roles(i + 1, 0)
                    store(i + 1, cols_of(0))
                else:
                    difference(i + 1, 0)
                gate_value(i + 1, 2)
                gate_value(i + 1, 3)
                if i + 3 < ROW_TILES:
                    part_h(i + 3, 1)
                difference(i + 1, 1)
                if i + 3 < ROW_TILES:
                    part_a(i + 3)
                if i + 1 == ROW_TILES - 1:
                    final_add(i + 1, cols_of(1), nc.gpsimd)
        open_output(7)
        logits(7, 0)
        role_product(7, 0)
        role_product(6, 3)
        gate_value(7, 0)
        difference(6, 2)
        difference(7, 0)
        difference(6, 3)
        hold_back(7, 0)
        final_add(6, slice(SLICE * 3, SLICE * 4), nc.gpsimd)
        final_add(6, slice(SLICE * 1, SLICE * 2), nc.gpsimd)
        final_add(6, slice(SLICE * 2, SLICE * 3), nc.gpsimd)
        logits(7, 1)
        role_product(7, 1)
        logits(7, 2)
        logits(7, 3)
        role_product(7, 2)
        gate_value(7, 1)
        from_roles(7, 0)
        store(7, cols_of(0))
        gate_value(7, 2)
        difference(7, 1)
        gate_value(7, 3)
        role_product(7, 3)
        difference(7, 2)
        final_add(7, slice(SLICE * 1, SLICE * 2), nc.vector)
        difference(7, 3)
        final_add(7, slice(SLICE * 2, SLICE * 3), nc.vector)
        final_add(7, slice(SLICE * 3, SLICE * 4), nc.vector)
